import numpy as np
import ml_dtypes


def mxq(x, axis, fmt="e4m3"):
    dtype, down = {"e4m3": (ml_dtypes.float8_e4m3fn, 7), "e5m2": (ml_dtypes.float8_e5m2, 14)}[fmt]
    v = np.moveaxis(np.asarray(x, np.float32).astype(ml_dtypes.bfloat16).astype(np.float64), axis, -1)
    blocks = v.reshape(v.shape[:-1] + (-1, 32))
    amax = np.abs(blocks).max(-1, keepdims=True)
    byte = np.maximum(np.where(amax > 0, np.frexp(amax)[1] - 1 + 127, 0) - down, 1)
    scale = np.exp2(byte - 127.0)
    codes = (blocks / scale).astype(np.float32).astype(dtype).astype(np.float64)
    return np.moveaxis((codes * scale).reshape(v.shape), -1, axis)


WIDE = False


def mx_kscale(k):
    if not WIDE:
        return np.ones(k)
    levels = np.array([18, -18])
    if k % 512:
        return np.exp2(np.random.permutation(np.resize(levels, k // 32))).repeat(32)
    a = np.empty((k // 512, 16))
    for p in range(k // 512):
        a[p, :8] = np.random.permutation(np.resize(levels, 8))
        for g in range(8):
            far = levels[np.abs(levels - a[p, g]) >= 10]
            a[p, g + 8] = far[np.random.randint(len(far))]
    return np.exp2(a.ravel()).repeat(32)


BF16 = ml_dtypes.bfloat16


def bf(x):
    return np.asarray(x, np.float32).astype(BF16)


def f64(x):
    return np.asarray(x).astype(np.float64)


B, N, C = 4, 512, 512
R = B * N
G = 3 * C


def sigmoid(v):
    return 1.0 / (1.0 + np.exp(-v))


def gru_forward(x_proj, annotations, recurrent_kernel, bias_h):
    b, n, c = annotations.shape
    h = f64(annotations).reshape(-1, c)
    mh = h @ f64(recurrent_kernel) + f64(bias_h)
    xz, xr, xh = np.split(f64(x_proj), 3, axis=-1)
    hz, hr, hc = np.split(mh, 3, axis=-1)
    z = sigmoid(xz + hz)
    r = sigmoid(xr + hr)
    cand = np.tanh(xh + r * hc)
    return mh, (z * h + (1.0 - z) * cand).reshape(b, n, c)


def setup_inputs():
    s = mx_kscale(R).reshape(B, N, 1)
    u = mx_kscale(G).reshape(-1, 32)[::3].reshape(-1)
    u = u / u.max()
    x_proj = bf(np.random.standard_normal((R, G)))
    h0 = bf(np.random.standard_normal((B, N, C)))
    w0 = bf(np.random.standard_normal((C, G)) / np.sqrt(C))
    bias_h = bf(np.random.standard_normal(G) * 0.3)
    g = bf(4.0 * np.random.standard_normal((B, N, C)) * np.exp2(np.random.randint(-6, 1, (B, N, 1))) / s * u)
    mh, h_new = gru_forward(x_proj, h0, w0, bias_h)
    return {"x_proj": x_proj,
            "annotations": bf(f64(h0) * s),
            "recurrent_kernel": bf(f64(w0) / np.tile(u, 3)),
            "bias_h": bias_h,
            "mh": np.asarray(mh, np.float32),
            "h_new": np.asarray(h_new, np.float32),
            "grad_out": g}


def reference(x_proj, annotations, recurrent_kernel, bias_h, mh, h_new, grad_out):
    b, n, c = annotations.shape
    h = f64(annotations).reshape(-1, c)
    hn = f64(h_new).reshape(-1, c)
    g = f64(grad_out).reshape(-1, c)
    xz, xr, xh = np.split(f64(x_proj), 3, axis=-1)
    hz, hr, hc = np.split(f64(mh), 3, axis=-1)
    z = sigmoid(xz + hz)
    r = sigmoid(xr + hr)
    cand = np.tanh(xh + r * hc)
    dc = g * (1.0 - z) * (1.0 - cand * cand)
    dzg = g * (hn - cand) * (1.0 - z)
    drg = dc * hc * r * (1.0 - r)
    dmh = np.concatenate([dzg, drg, dc * r], axis=1)
    prod = mxq(dmh, 1, "e5m2") @ mxq(f64(recurrent_kernel), 1, "e4m3").T
    dh = prod + g * z
    dw = mxq(h, 0, "e4m3").T @ mxq(dmh, 0, "e5m2")
    return dh.reshape(b, n, c), dw

@@ -1,0 +1,527 @@
+from contextlib import ExitStack
+
+import concourse.mybir as mybir
+from concourse.masks import make_identity
+
+TOKENS, C, G = 2048, 512, 1536
+FLOPS = 2 * 2 * TOKENS * C * G
+BYTES = TOKENS * G * 6 + TOKENS * C * 8 + C * G * 2 + TOKENS * C * 4 + C * G * 4
+
+F32 = mybir.dt.float32
+BF16 = mybir.dt.bfloat16
+U32 = mybir.dt.uint32
+U8 = mybir.dt.uint8
+E4X4 = mybir.dt.float8_e4m3fn_x4
+E5X4 = mybir.dt.float8_e5m2_x4
+ACT = mybir.ActivationFunctionType
+OP = mybir.AluOpType
+
+P = 128
+GROUPS = 4
+CHUNKS = 8
+J = 2
+Z, R, H = 0, 1, 2
+
+
+def gate(q):
+    return slice(q * C, (q + 1) * C)
+
+
+def tile_gatedgraphconvolution_pb_v_kernel(
+    tc, x_proj, annotations, recurrent_kernel, bias_h, mh, h_new, grad_out, out_0, out_1
+):
+    nc = tc.nc
+    x_v = x_proj.rearrange("(g p j) w -> g p j w", g=GROUPS, j=4)
+    mh_v = mh.rearrange("(g p j) w -> g p j w", g=GROUPS, j=4)
+    hn_v = h_new.rearrange("g (p j) w -> g p j w", j=4)
+    g_v = grad_out.rearrange("g (p j) w -> g p j w", j=4)
+    h_v = annotations.rearrange("g (p j) w -> g p j w", j=4)
+    o_v = out_0.rearrange("g (p j) w -> g p j w", j=4)
+    w_v = recurrent_kernel.rearrange("(b p) w -> p b w", p=P)
+
+    with ExitStack() as ctx:
+        keep = ctx.enter_context(tc.tile_pool(name="keep", bufs=1))
+        inp = ctx.enter_context(tc.tile_pool(name="inp", bufs=3))
+        mid = ctx.enter_context(tc.tile_pool(name="mid", bufs=1))
+        mx = ctx.enter_context(tc.tile_pool(name="mx", bufs=2))
+        psum = ctx.enter_context(tc.psum_pool(name="psum", bufs=2))
+
+        id_f = keep.tile([P, P], F32, name="id_f")
+        id_b = keep.tile([P, P], BF16, name="id_b")
+        warm = keep.tile([P, 1], F32, name="warm")
+        make_identity(nc, id_f[:])
+        make_identity(nc, id_b[:])
+        nc.vector.memset(warm[:], 0.0)
+        nc.scalar.activation(out=warm[:], in_=warm[:], func=ACT.Sigmoid)
+
+        w_codes, w_scales, tok_codes, tok_scales, h_codes, h_scales = {}, {}, {}, {}, {}, {}
+        for q in range(3):
+            w_codes[q] = keep.tile([P, C], U32, name="w_codes%d" % q, align_bytes=64)
+            w_scales[q] = keep.tile([P, C], U8, name="w_scales%d" % q, align_bytes=64)
+        for g in range(GROUPS):
+            h_codes[g] = keep.tile([P, C], U32, name="h_codes%d" % g, align_bytes=64)
+            h_scales[g] = keep.tile([P, C], U8, name="h_scales%d" % g, align_bytes=64)
+            for q in range(3):
+                tok_codes[g, q] = keep.tile([P, C], U32, name="tok_codes%d_%d" % (g, q), align_bytes=64)
+                tok_scales[g, q] = keep.tile([P, C], U8, name="tok_scales%d_%d" % (g, q), align_bytes=64)
+
+        t = {}
+
+        def alloc_in(i):
+            t["x", i] = inp.tile([P, J, G], BF16, name="x", tag="x")
+            t["mh", i] = inp.tile([P, J, G], F32, name="mh", tag="mh")
+            t["g", i] = inp.tile([P, J, C], BF16, name="gin", tag="g")
+            t["hn", i] = inp.tile([P, J, C], F32, name="hn", tag="hn")
+
+        def rows(i):
+            return i // 2, slice((i % 2) * J, (i % 2) * J + J)
+
+        def load(i):
+            g, js = rows(i)
+            nc.sync.dma_start(out=t["mh", i][:], in_=mh_v[g][:, js, :])
+            nc.sync.dma_start(out=t["x", i][:], in_=x_v[g][:, js, :])
+            nc.sync.dma_start(out=t["g", i][:], in_=g_v[g][:, js, :])
+            nc.sync.dma_start(out=t["hn", i][:], in_=hn_v[g][:, js, :])
+
+        def load_first():
+            for j in range(J):
+                nc.sync.dma_start(out=t["mh", 0][:, j, gate(R)], in_=mh_v[0][:, j, gate(R)])
+                nc.sync.dma_start(out=t["x", 0][:, j, gate(R)], in_=x_v[0][:, j, gate(R)])
+            for q in (H, Z):
+                nc.sync.dma_start(out=t["mh", 0][:, :, gate(q)], in_=mh_v[0][:, 0:J, gate(q)])
+                nc.sync.dma_start(out=t["x", 0][:, :, gate(q)], in_=x_v[0][:, 0:J, gate(q)])
+            nc.sync.dma_start(out=t["hn", 0][:], in_=hn_v[0][:, 0:J, :])
+            nc.sync.dma_start(out=t["g", 0][:], in_=g_v[0][:, 0:J, :])
+
+        def load_h(g):
+            t["h", g] = inp.tile([P, 4, C], BF16, name="h", tag="h", bufs=1)
+            nc.sync.dma_start(out=t["h", g][:], in_=h_v[g])
+
+        def tt(out, a, b, op):
+            nc.vector.tensor_tensor(out=out, in0=a, in1=b, op=op)
+
+        def stt(out, a, s, b, op0, op1):
+            nc.vector.scalar_tensor_tensor(out=out, in0=a, scalar=s, in1=b, op0=op0, op1=op1)
+
+        ALL = slice(0, J)
+
+        def gate_tile(k, i):
+            t[k, i] = mid.tile([P, J, C], F32, name=k, tag=k, bufs=2)
+
+        def pe_add(k, q, i, j):
+            bank = psum.tile([P, C], F32, name="pa", tag="pa", bufs=4)
+            t["pa", k, i, j] = bank
+            nc.tensor.matmul(bank[:], lhsT=id_b[:], rhs=t["x", i][:, j, gate(q)], start=True, stop=False)
+            nc.tensor.matmul(bank[:], lhsT=id_f[:], rhs=t["mh", i][:, j, gate(q)], start=False, stop=True)
+
+        def v_add(k, q, i, js=ALL):
+            tt(t[k, i][:, js, :], t["x", i][:, js, gate(q)], t["mh", i][:, js, gate(q)], OP.add)
+
+        def sig(k, i, js=ALL):
+            nc.scalar.activation(
+                out=t[k, i][:, js, :], in_=t[k, i][:, js, :], func=ACT.Sigmoid, scale=-1.0 if k == "q" else 1.0
+            )
+
+        def sig_pe(k, i, j):
+            nc.scalar.activation(
+                out=t[k, i][:, j, :], in_=t["pa", k, i, j][:], func=ACT.Sigmoid, scale=-1.0 if k == "q" else 1.0
+            )
+
+        def mid_tiles(i):
+            t["c", i] = mid.tile([P, J, C], F32, name="c", tag="c")
+            if i < CHUNKS - 1:
+                t["t1", i] = mid.tile([P, J, C], F32, name="t1", tag="t1")
+                t["gq", i] = mid.tile([P, J, C], F32, name="gq", tag="gq")
+                t["c2", i] = mid.tile([P, J, C], F32, name="c2", tag="c2")
+            else:
+                t["t1", i] = inp.tile([P, J, C], F32, name="t1", tag="hn")
+                t["gq", i] = inp.tile([P, J, C], F32, name="gq", tag="x")
+                t["c2", i] = inp.tile([P, J, C], F32, name="c2", tag="hn")
+
+        def f_t1(i, js=ALL):
+            tt(t["t1", i][:, js, :], t["r", i][:, js, :], t["mh", i][:, js, gate(H)], OP.mult)
+
+        def f_ac(i, js=ALL):
+            tt(t["c", i][:, js, :], t["x", i][:, js, gate(H)], t["t1", i][:, js, :], OP.add)
+
+        def f_gq(i, js=ALL):
+            tt(t["gq", i][:, js, :], t["g", i][:, js, :], t["q", i][:, js, :], OP.mult)
+
+        def f_gz(i):
+            t["gz", i] = mid.tile([P, J, C], F32, name="gz", tag="gz", bufs=2)
+            tt(t["gz", i][:], t["g", i][:], t["gq", i][:], OP.subtract)
+
+        def f_v(i):
+            stt(t["t1", i][:], t["r", i][:], 1.0, t["t1", i][:], OP.subtract, OP.mult)
+
+        def tanh(i, js=ALL):
+            nc.scalar.activation(out=t["c", i][:, js, :], in_=t["c", i][:, js, :], func=ACT.Tanh)
+
+        def square(i, js=ALL):
+            nc.scalar.activation(out=t["c2", i][:, js, :], in_=t["c", i][:, js, :], func=ACT.Square)
+
+        def f_hm(i):
+            tt(t["c", i][:], t["hn", i][:], t["c", i][:], OP.subtract)
+
+        def dz_tiles(g):
+            for q in range(3):
+                t["dz", g, q] = mx.tile([P, 4, C], BF16, name="dz%d" % q, tag="dz%d" % q)
+
+        def f_ndc(i):
+            stt(t["c2", i][:], t["c2", i][:], 1.0, t["gq", i][:], OP.subtract, OP.mult)
+
+        def f_dzg(i):
+            g, js = rows(i)
+            tt(t["dz", g, Z][:, js, :], t["c", i][:], t["gq", i][:], OP.mult)
+
+        def f_dcr(i):
+            g, js = rows(i)
+            stt(t["dz", g, H][:, js, :], t["c2", i][:], -1.0, t["r", i][:], OP.mult, OP.mult)
+
+        def f_drg(i):
+            g, js = rows(i)
+            tt(t["dz", g, R][:, js, :], t["c2", i][:], t["t1", i][:], OP.mult)
+
+        def transpose(i, q):
+            g, js = rows(i)
+            bank = psum.tile([P, 2, 2 * P], F32, name="tr", tag="tr", bufs=2)
+            t["tr", i, q] = bank
+            for j in range(J):
+                words = t["dz", g, q][:, js.start + j, :].bitcast(F32)
+                for u in range(2):
+                    nc.tensor.transpose(bank[:, u, j * P : (j + 1) * P], words[:, u : C // 2 : 2], id_f[:])
+
+        def evac(i, q):
+            t["dzT", i, q] = mx.tile([P, 2 * P, 4], BF16, name="dzT", tag="dzT", bufs=4, align_bytes=64)
+            nc.scalar.copy(out=t["dzT", i, q][:].bitcast(F32), in_=t["tr", i, q][:].rearrange("p u r -> p r u"))
+
+        def quant_f(i, q):
+            codes = mx.tile([P, 2 * P], U32, name="f_codes", tag="f_codes", bufs=6, align_bytes=64)
+            scales = mx.tile([P, 2 * P], U8, name="f_scales", tag="f_scales", bufs=6, align_bytes=64)
+            t["fc", i, q], t["fs", i, q] = codes, scales
+            nc.vector.quantize_mx(
+                out=codes[:].bitcast(E5X4), scales=scales[:], in_=t["dzT", i, q][:].rearrange("p r t -> p (r t)")
+            )
+
+        def mm_0_tile(i, j, gates, first, last):
+            if first:
+                t["o0", i, j] = psum.tile([P, C], F32, name="o0", tag="o0", bufs=2)
+            cols = slice(j * P, (j + 1) * P)
+            for n, q in enumerate(gates):
+                nc.tensor.matmul_mx(
+                    t["o0", i, j][:],
+                    lhsT=t["fc", i, q][:, cols].bitcast(E5X4),
+                    lhsT_scale=t["fs", i, q][:, cols],
+                    rhs=w_codes[q][:].bitcast(E4X4),
+                    rhs_scale=w_scales[q][:],
+                    start=(first and n == 0),
+                    stop=(last and n == len(gates) - 1),
+                )
+
+        def mm_0(i):
+            for j in range(J):
+                mm_0_tile(i, j, (Z, H, R), True, True)
+
+        def fin_0(i):
+            g, js = rows(i)
+            res = mid.tile([P, J, C], F32, name="res", tag="res", bufs=2)
+            for j in range(J):
+                tt(res[:, j, :], t["o0", i, j][:], t["gz", i][:, j, :], OP.add)
+            nc.sync.dma_start(out=o_v[g][:, js, :], in_=res[:])
+
+        def interleave(copy, src, key, cols=slice(0, C)):
+            if key not in t:
+                t[key] = mx.tile([P, C, 4], BF16, name="ilv", tag="ilv", bufs=3, align_bytes=64)
+            copy(out=t[key][:, cols, :], in_=src[:, :, cols].rearrange("p j w -> p w j"))
+
+        def quant_t(key, codes, scales, dt):
+            nc.vector.quantize_mx(
+                out=codes[:].bitcast(dt), scales=scales[:], in_=t[key][:].rearrange("p w j -> p (w j)")
+            )
+
+        def ilv_dz(g, q):
+            interleave(nc.scalar.copy, t["dz", g, q], ("ilv", g, q))
+
+        def quant_dz(g, q):
+            quant_t(("ilv", g, q), tok_codes[g, q], tok_scales[g, q], E5X4)
+
+        def ilv_h(g):
+            interleave(nc.scalar.copy, t["h", g], ("ilvh", g))
+
+        def quant_h(g):
+            quant_t(("ilvh", g), h_codes[g], h_scales[g], E4X4)
+
+        def mm_1(q, m, g, bank, start, stop):
+            cols = slice(m * P, (m + 1) * P)
+            nc.tensor.matmul_mx(
+                bank[:],
+                lhsT=h_codes[g][:, cols].bitcast(E4X4),
+                lhsT_scale=h_scales[g][:, cols],
+                rhs=tok_codes[g, q][:].bitcast(E5X4),
+                rhs_scale=tok_scales[g, q][:],
+                start=start,
+                stop=stop,
+            )
+
+        def fin_1(q, m, bank):
+            if m == 0:
+                t["res", q] = inp.tile([P, 4, C], F32, name="res1", tag="mh")
+            nc.scalar.copy(out=t["res", q][:, m, :], in_=bank[:])
+
+        def add_1(q, m, bank):
+            tt(t["res", q][:, m, :], bank[:], t["res", q][:, m, :], OP.add)
+
+        def store_1(q, m):
+            nc.sync.dma_start(out=out_1[m * P : (m + 1) * P, gate(q)], in_=t["res", q][:, m, :])
+
+        def pass_1(q, groups, first, last, ms=range(4), tag="pa"):
+            for m in ms:
+                if first:
+                    t["b1", q, m] = psum.tile([P, C], F32, name="pa", tag=tag, bufs=4 if tag == "pa" else 2)
+                for n, gg in enumerate(groups):
+                    mm_1(q, m, gg, t["b1", q, m], first and n == 0, last and n == len(groups) - 1)
+
+        def w_transpose(q, half):
+            bank = psum.tile([P, 2, 2 * P], F32, name="tr", tag="tr", bufs=2)
+            for b in range(2):
+                words = t["w"][:, 2 * half + b, gate(q)].bitcast(F32)
+                for u in range(2):
+                    nc.tensor.transpose(bank[:, u, b * P : (b + 1) * P], words[:, u : C // 2 : 2], id_f[:])
+            if half == 0:
+                t["wT", q] = mx.tile([P, C, 4], BF16, name="ilv", tag="ilv", bufs=3, align_bytes=64)
+            nc.scalar.copy(
+                out=t["wT", q][:, half * 2 * P : (half + 1) * 2 * P, :].bitcast(F32),
+                in_=bank[:].rearrange("p u r -> p r u"),
+            )
+
+        def w_quant(q):
+            quant_t(("wT", q), w_codes[q], w_scales[q], E4X4)
+
+        with tc.manual_schedule():
+            pe_r = {2: (0, 1), 4: (0, 1), 6: (0,)}
+            alloc_in(0)
+            t["w"] = inp.tile([P, 4, G], BF16, name="w", tag="mh")
+            alloc_in(1)
+            load_first()
+            load(1)
+            nc.sync.dma_start(out=t["w"][:], in_=w_v)
+
+            gate_tile("r", 0)
+            gate_tile("q", 0)
+            mid_tiles(0)
+            for j in range(J):
+                v_add("r", R, 0, j)
+                sig("r", 0, j)
+            for j in range(J):
+                f_t1(0, j)
+            for j in range(J):
+                f_ac(0, j)
+                tanh(0, j)
+            square(0)
+            for j in range(J):
+                v_add("q", Z, 0, j)
+                sig("q", 0, j)
+            f_v(0)
+            alloc_in(2)
+            load(2)
+            load_h(0)
+
+            def next_pe(nxt):
+                for j in pe_r.get(nxt, ()):
+                    pe_add("r", R, nxt, j)
+                for j in range(J):
+                    pe_add("q", Z, nxt, j)
+
+            def next_v(nxt):
+                on_pe = pe_r.get(nxt, ())
+                on_v = [j for j in range(J) if j not in on_pe]
+                if len(on_v) == 2:
+                    v_add("r", R, nxt)
+                    sig("r", nxt)
+                else:
+                    for j in on_v:
+                        v_add("r", R, nxt, j)
+                        sig("r", nxt, j)
+                for j in on_pe:
+                    sig_pe("r", nxt, j)
+                for j in range(J):
+                    sig_pe("q", nxt, j)
+
+            for i in range(CHUNKS - 2):
+                g, h = i // 2, i % 2
+                last, nxt = i - 1, i + 1
+                if i > 1:
+                    alloc_in(i + 2)
+                    load(i + 2)
+                if last >= 0:
+                    transpose(last, R)
+                    evac(last, R)
+                gate_tile("r", nxt)
+                gate_tile("q", nxt)
+                if h == 0:
+                    dz_tiles(g)
+                if i == 0:
+                    next_pe(nxt)
+                    f_hm(i)
+                    f_gq(i)
+                    f_ndc(i)
+                    f_gz(i)
+                    f_dzg(i)
+                    next_v(nxt)
+                    f_dcr(i)
+                    f_drg(i)
+                else:
+                    mid_tiles(i)
+                    f_gq(i)
+                    quant_f(last, Z)
+                    f_t1(i)
+                    if i == 2:
+                        for q in range(3):
+                            w_quant(q)
+                        mm_0(0)
+                    if i == 2:
+                        f_ac(i)
+                        quant_f(last, H)
+                        fin_0(0)
+                        f_gz(i)
+                    else:
+                        f_gz(i)
+                        f_ac(i)
+                        quant_f(last, H)
+                    f_v(i)
+                    if h == 0:
+                        ilv_dz(g - 1, Z)
+                    elif g > 0:
+                        ilv_dz(g - 1, R)
+                    tanh(i)
+                    square(i)
+                    next_pe(nxt)
+                    quant_f(last, R)
+                    next_v(nxt)
+                    if i == 1:
+                        for q in range(3):
+                            w_transpose(q, 0)
+                            w_transpose(q, 1)
+                        alloc_in(3)
+                        load(3)
+                    if i > 2:
+                        quant_h(i - 3)
+                    if h == 0:
+                        quant_dz(g - 1, Z)
+                        ilv_dz(g - 1, H)
+                    elif g > 0:
+                        quant_dz(g - 1, H)
+                        quant_dz(g - 1, R)
+                    f_hm(i)
+                    if i > 1:
+                        mm_0(last)
+                        fin_0(last)
+                    if i > 1:
+                        ilv_h(i - 2)
+                        if i < 5:
+                            load_h(i - 1)
+                    f_ndc(i)
+                    f_dzg(i)
+                    f_dcr(i)
+                    f_drg(i)
+                for q in (Z, H):
+                    transpose(i, q)
+                    evac(i, q)
+
+            g, a, b = GROUPS - 1, CHUNKS - 2, CHUNKS - 1
+            transpose(a - 1, R)
+            evac(a - 1, R)
+            gate_tile("r", b)
+            gate_tile("q", b)
+            dz_tiles(g)
+            mid_tiles(a)
+            f_gq(a)
+            quant_f(a - 1, Z)
+            f_t1(a)
+            quant_f(a - 1, H)
+            f_ac(a)
+            ilv_dz(g - 1, Z)
+            tanh(a)
+            square(a)
+            next_pe(b)
+            quant_f(a - 1, R)
+            f_gz(a)
+            quant_h(g)
+            next_v(b)
+            quant_dz(g - 1, Z)
+            ilv_dz(g - 1, H)
+            f_hm(a)
+            mm_0(a - 1)
+            fin_0(a - 1)
+            f_dzg(a)
+            transpose(a, Z)
+            evac(a, Z)
+            ilv_dz(g - 1, R)
+
+            mid_tiles(b)
+            f_gq(b)
+            f_t1(b)
+            quant_dz(g - 1, H)
+            f_ac(b)
+            tanh(b)
+            square(b)
+            f_ndc(a)
+            quant_dz(g - 1, R)
+            pass_1(R, range(3), True, True)
+            quant_f(a, Z)
+            f_v(a)
+            f_hm(b)
+            for m in range(4):
+                fin_1(R, m, t["b1", R, m])
+            pass_1(Z, range(3), True, False)
+            f_dcr(a)
+            f_dzg(b)
+            transpose(b, Z)
+            transpose(a, H)
+            ilv_dz(g, Z)
+            evac(b, Z)
+            evac(a, H)
+            f_ndc(b)
+            f_gz(b)
+            f_dcr(b)
+            transpose(b, H)
+            quant_dz(g, Z)
+            pass_1(Z, (3,), False, True)
+            quant_f(b, Z)
+            quant_f(a, H)
+            evac(b, H)
+            for m in range(4):
+                fin_1(Z, m, t["b1", Z, m])
+                store_1(Z, m)
+            for j in range(J):
+                mm_0_tile(a, j, (Z, H), True, False)
+            pass_1(H, range(3), True, False, (0, 1))
+            ilv_dz(g, H)
+            f_v(b)
+            f_drg(a)
+            transpose(a, R)
+            quant_f(b, H)
+            f_drg(b)
+            transpose(b, R)
+            pass_1(H, range(3), True, False, (2, 3))
+            evac(a, R)
+            interleave(nc.scalar.copy, t["dz", g, R], ("ilv", g, R), slice(0, 192))
+            interleave(nc.vector.tensor_copy, t["dz", g, R], ("ilv", g, R), slice(192, C))
+            quant_f(a, R)
+            evac(b, R)
+            quant_dz(g, H)
+            for j in range(J):
+                mm_0_tile(a, j, (R,), False, True)
+            pass_1(H, (3,), False, True)
+            quant_dz(g, R)
+            quant_f(b, R)
+            for m in range(4):
+                fin_1(H, m, t["b1", H, m])
+                store_1(H, m)
+            fin_0(a)
+            for m in range(4):
+                pass_1(R, (3,), True, True, (m,), "tr" if m < 2 else "pa")
+                add_1(R, m, t["b1", R, m])
+                store_1(R, m)
+            mm_0(b)
+            fin_0(b)

@@ -93,6 +93,20 @@ def tile_gatedgraphconvolution_pb_v_kernel(
             nc.sync.dma_start(out=t["hn", 0][:], in_=hn_v[0][:, 0:J, :])
             nc.sync.dma_start(out=t["g", 0][:], in_=g_v[0][:, 0:J, :])
 
+        def load_gates(i, gates):
+            g, js = rows(i)
+            for q in gates:
+                nc.sync.dma_start(out=t["mh", i][:, :, gate(q)], in_=mh_v[g][:, js, gate(q)])
+                nc.sync.dma_start(out=t["x", i][:, :, gate(q)], in_=x_v[g][:, js, gate(q)])
+
+        def load_g(i):
+            g, js = rows(i)
+            nc.sync.dma_start(out=t["g", i][:], in_=g_v[g][:, js, :])
+
+        def load_hn(i):
+            g, js = rows(i)
+            nc.sync.dma_start(out=t["hn", i][:], in_=hn_v[g][:, js, :])
+
         def load_h(g):
             t["h", g] = inp.tile([P, 4, C], BF16, name="h", tag="h", bufs=1)
             nc.sync.dma_start(out=t["h", g][:], in_=h_v[g])
@@ -113,6 +127,32 @@ def tile_gatedgraphconvolution_pb_v_kernel(
             t["pa", k, i, j] = bank
             nc.tensor.matmul(bank[:], lhsT=id_b[:], rhs=t["x", i][:, j, gate(q)], start=True, stop=False)
             nc.tensor.matmul(bank[:], lhsT=id_f[:], rhs=t["mh", i][:, j, gate(q)], start=False, stop=True)
+
+        def z_sum(i, j):
+            bank = psum.tile([P, 4, P], F32, name="pa", tag="pa", bufs=4)
+            t["z1", i, j] = bank
+            for b in range(4):
+                cols = slice(b * P, (b + 1) * P)
+                nc.tensor.matmul(
+                    bank[:, b, :], lhsT=t["mh", i][:, j, cols], rhs=id_f[:], start=(b == 0), stop=False, is_transpose=True
+                )
+            for b in range(4):
+                cols = slice(b * P, (b + 1) * P)
+                nc.tensor.matmul(bank[:, b, :], lhsT=t["x", i][:, j, cols], rhs=id_b[:], start=False, stop=(b == 3))
+
+        def z_sig(i, j):
+            nc.scalar.activation(
+                out=t["q", i][:, j, :],
+                in_=t["z1", i, j][:].rearrange("p b k -> p (b k)"),
+                func=ACT.Sigmoid,
+                scale=-1.0,
+            )
+
+        def z_back(i, j):
+            bank = psum.tile([P, 4, P], F32, name="pa", tag="pa", bufs=4)
+            t["z2", i, j] = bank
+            for b in range(4):
+                nc.tensor.transpose(bank[:, b, :], t["q", i][:, j, b * P : (b + 1) * P], id_f[:])
 
         def v_add(k, q, i, js=ALL):
             tt(t[k, i][:, js, :], t["x", i][:, js, gate(q)], t["mh", i][:, js, gate(q)], OP.add)
@@ -145,10 +185,19 @@ def tile_gatedgraphconvolution_pb_v_kernel(
             tt(t["c", i][:, js, :], t["x", i][:, js, gate(H)], t["t1", i][:, js, :], OP.add)
 
         def f_gq(i, js=ALL):
+            if ("z2", i, 0) in t:
+                for j in range(J):
+                    tt(
+                        t["gq", i][:, j, :],
+                        t["z2", i, j][:].rearrange("p b k -> p (b k)"),
+                        t["g", i][:, j, :],
+                        OP.mult,
+                    )
+                return
             tt(t["gq", i][:, js, :], t["g", i][:, js, :], t["q", i][:, js, :], OP.mult)
 
         def f_gz(i):
-            t["gz", i] = mid.tile([P, J, C], F32, name="gz", tag="gz", bufs=2)
+            t["gz", i] = mid.tile([P, J, C], F32, name="gz", tag="gz", bufs=3)
             tt(t["gz", i][:], t["g", i][:], t["gq", i][:], OP.subtract)
 
         def f_v(i):
@@ -196,8 +245,8 @@ def tile_gatedgraphconvolution_pb_v_kernel(
             nc.scalar.copy(out=t["dzT", i, q][:].bitcast(F32), in_=t["tr", i, q][:].rearrange("p u r -> p r u"))
 
         def quant_f(i, q):
-            codes = mx.tile([P, 2 * P], U32, name="f_codes", tag="f_codes", bufs=6, align_bytes=64)
-            scales = mx.tile([P, 2 * P], U8, name="f_scales", tag="f_scales", bufs=6, align_bytes=64)
+            codes = mx.tile([P, 2 * P], U32, name="f_codes", tag="f_codes", bufs=9, align_bytes=64)
+            scales = mx.tile([P, 2 * P], U8, name="f_scales", tag="f_scales", bufs=9, align_bytes=64)
             t["fc", i, q], t["fs", i, q] = codes, scales
             nc.vector.quantize_mx(
                 out=codes[:].bitcast(E5X4), scales=scales[:], in_=t["dzT", i, q][:].rearrange("p r t -> p (r t)")
@@ -224,10 +273,14 @@ def tile_gatedgraphconvolution_pb_v_kernel(
 
         def fin_0(i):
             g, js = rows(i)
-            res = mid.tile([P, J, C], F32, name="res", tag="res", bufs=2)
             for j in range(J):
-                tt(res[:, j, :], t["o0", i, j][:], t["gz", i][:, j, :], OP.add)
-            nc.sync.dma_start(out=o_v[g][:, js, :], in_=res[:])
+                tt(t["gz", i][:, j, :], t["o0", i, j][:], t["gz", i][:, j, :], OP.add)
+            nc.sync.dma_start(out=o_v[g][:, js, :], in_=t["gz", i][:])
+
+        def fin_0j(i, j):
+            g, js = rows(i)
+            tt(t["gz", i][:, j, :], t["o0", i, j][:], t["gz", i][:, j, :], OP.add)
+            nc.sync.dma_start(out=o_v[g][:, js.start + j, :], in_=t["gz", i][:, j, :])
 
         def interleave(copy, src, key, cols=slice(0, C)):
             if key not in t:
@@ -288,7 +341,7 @@ def tile_gatedgraphconvolution_pb_v_kernel(
                 for u in range(2):
                     nc.tensor.transpose(bank[:, u, b * P : (b + 1) * P], words[:, u : C // 2 : 2], id_f[:])
             if half == 0:
-                t["wT", q] = mx.tile([P, C, 4], BF16, name="ilv", tag="ilv", bufs=3, align_bytes=64)
+                t["wT", q] = mx.tile([P, C, 4], BF16, name="wT", tag="wT", bufs=3, align_bytes=64)
             nc.scalar.copy(
                 out=t["wT", q][:, half * 2 * P : (half + 1) * 2 * P, :].bitcast(F32),
                 in_=bank[:].rearrange("p u r -> p r u"),
@@ -297,15 +350,65 @@ def tile_gatedgraphconvolution_pb_v_kernel(
         def w_quant(q):
             quant_t(("wT", q), w_codes[q], w_scales[q], E4X4)
 
-        with tc.manual_schedule():
-            pe_r = {2: (0, 1), 4: (0, 1), 6: (0,)}
-            alloc_in(0)
-            t["w"] = inp.tile([P, 4, G], BF16, name="w", tag="mh")
-            alloc_in(1)
-            load_first()
-            load(1)
-            nc.sync.dma_start(out=t["w"][:], in_=w_v)
+        pe_r = {1: (0,),2: (0,1),3: (0,1),4: (0,1),5: (0,1),6: (0,1),7: (0,)}
 
+        def tiles_g(i):
+            gate_tile("r", i + 1)
+            gate_tile("q", i + 1)
+            if i % 2 == 0:
+                dz_tiles(i // 2)
+            if i > 0:
+                mid_tiles(i)
+
+        def r_v(n):
+            js = [j for j in range(J) if j not in pe_r.get(n, ())]
+            if len(js) == J:
+                v_add("r", R, n)
+            else:
+                for j in js:
+                    v_add("r", R, n, j)
+
+        def r_sig(n):
+            js = [j for j in range(J) if j not in pe_r.get(n, ())]
+            if len(js) == J:
+                sig("r", n)
+            else:
+                for j in js:
+                    sig("r", n, j)
+
+        def r_pe(n):
+            for j in pe_r.get(n, ()):
+                pe_add("r", R, n, j)
+
+        def r_sigpe(n):
+            for j in pe_r.get(n, ()):
+                sig_pe("r", n, j)
+
+        def ilvq(g, q, k):
+            w = C // 2
+            interleave(nc.scalar.copy, t["dz", g, q], ("ilv", g, q), slice(k * w, k * w + w))
+
+        def ilvv(g, q, k):
+            w = C // 2
+            interleave(nc.vector.tensor_copy, t["dz", g, q], ("ilv", g, q), slice(k * w, k * w + w))
+
+        def ilvh(g, k):
+            w = C // 2
+            interleave(nc.scalar.copy, t["h", g], ("ilvh", g), slice(k * w, k * w + w))
+
+        A, B = CHUNKS - 2, CHUNKS - 1
+        g = GROUPS - 1
+
+        with tc.manual_schedule():
+            alloc_in(0)
+            alloc_in(1)
+            alloc_in(2)
+            load_first()
+            load_gates(1, (Z, R))
+            load_g(1)
+            load_gates(1, (H,))
+            load_hn(1)
+            load_gates(2, (Z, R, H))
             gate_tile("r", 0)
             gate_tile("q", 0)
             mid_tiles(0)
@@ -322,206 +425,259 @@ def tile_gatedgraphconvolution_pb_v_kernel(
                 v_add("q", Z, 0, j)
                 sig("q", 0, j)
             f_v(0)
-            alloc_in(2)
-            load(2)
+            t["w"] = inp.tile([P, 4, G], BF16, name="w", tag="mh")
+            nc.sync.dma_start(out=t["w"][:], in_=w_v)
+            load_g(2)
+            load_hn(2)
             load_h(0)
-
-            def next_pe(nxt):
-                for j in pe_r.get(nxt, ()):
-                    pe_add("r", R, nxt, j)
-                for j in range(J):
-                    pe_add("q", Z, nxt, j)
-
-            def next_v(nxt):
-                on_pe = pe_r.get(nxt, ())
-                on_v = [j for j in range(J) if j not in on_pe]
-                if len(on_v) == 2:
-                    v_add("r", R, nxt)
-                    sig("r", nxt)
-                else:
-                    for j in on_v:
-                        v_add("r", R, nxt, j)
-                        sig("r", nxt, j)
-                for j in on_pe:
-                    sig_pe("r", nxt, j)
-                for j in range(J):
-                    sig_pe("q", nxt, j)
-
-            for i in range(CHUNKS - 2):
-                g, h = i // 2, i % 2
-                last, nxt = i - 1, i + 1
-                if i > 1:
-                    alloc_in(i + 2)
-                    load(i + 2)
-                if last >= 0:
-                    transpose(last, R)
-                    evac(last, R)
-                gate_tile("r", nxt)
-                gate_tile("q", nxt)
-                if h == 0:
-                    dz_tiles(g)
-                if i == 0:
-                    next_pe(nxt)
-                    f_hm(i)
-                    f_gq(i)
-                    f_ndc(i)
-                    f_gz(i)
-                    f_dzg(i)
-                    next_v(nxt)
-                    f_dcr(i)
-                    f_drg(i)
-                else:
+            i = 0
+            gate_tile("r", i + 1)
+            gate_tile("q", i + 1)
+            if i % 2 == 0:
+                dz_tiles(i // 2)
+            if i > 0:
+                mid_tiles(i)
+            f_hm(i)
+            f_gq(i)
+            z_sum(i + 1, 0)
+            f_dzg(i)
+            z_sig(i + 1, 0)
+            r_v(i + 1)
+            r_pe(i + 1)
+            f_ndc(i)
+            r_sigpe(i + 1)
+            z_sum(i + 1, 1)
+            z_sig(i + 1, 1)
+            f_gz(i)
+            r_sig(i + 1)
+            f_dcr(i)
+            transpose(i, Z)
+            transpose(i, H)
+            evac(i, Z)
+            evac(i, H)
+            z_back(i + 1, 1)
+            z_back(i + 1, 0)
+            f_drg(i)
+            for i in range(1, CHUNKS - 2):
+                gate_tile("r", i + 1)
+                gate_tile("q", i + 1)
+                if i % 2 == 0:
+                    dz_tiles(i // 2)
+                if i > 0:
                     mid_tiles(i)
-                    f_gq(i)
-                    quant_f(last, Z)
-                    f_t1(i)
-                    if i == 2:
-                        for q in range(3):
-                            w_quant(q)
-                        mm_0(0)
-                    if i == 2:
-                        f_ac(i)
-                        quant_f(last, H)
-                        fin_0(0)
-                        f_gz(i)
-                    else:
-                        f_gz(i)
-                        f_ac(i)
-                        quant_f(last, H)
-                    f_v(i)
-                    if h == 0:
-                        ilv_dz(g - 1, Z)
-                    elif g > 0:
-                        ilv_dz(g - 1, R)
-                    tanh(i)
-                    square(i)
-                    next_pe(nxt)
-                    quant_f(last, R)
-                    next_v(nxt)
-                    if i == 1:
-                        for q in range(3):
-                            w_transpose(q, 0)
-                            w_transpose(q, 1)
-                        alloc_in(3)
-                        load(3)
-                    if i > 2:
-                        quant_h(i - 3)
-                    if h == 0:
-                        quant_dz(g - 1, Z)
-                        ilv_dz(g - 1, H)
-                    elif g > 0:
-                        quant_dz(g - 1, H)
-                        quant_dz(g - 1, R)
-                    f_hm(i)
-                    if i > 1:
-                        mm_0(last)
-                        fin_0(last)
-                    if i > 1:
-                        ilv_h(i - 2)
-                        if i < 5:
-                            load_h(i - 1)
-                    f_ndc(i)
-                    f_dzg(i)
-                    f_dcr(i)
-                    f_drg(i)
-                for q in (Z, H):
-                    transpose(i, q)
-                    evac(i, q)
-
-            g, a, b = GROUPS - 1, CHUNKS - 2, CHUNKS - 1
-            transpose(a - 1, R)
-            evac(a - 1, R)
-            gate_tile("r", b)
-            gate_tile("q", b)
+                transpose(i - 1, R)
+                f_t1(i)
+                f_gq(i)
+                evac(i - 1, R)
+                if i % 2 == 0 and i > 1:
+                    ilvq(i // 2 - 1, Z, 1)
+                z_sum(i + 1, 1)
+                r_sig(i + 1)
+                f_ac(i)
+                r_v(i + 1)
+                quant_f(i - 1, Z)
+                if i > 2:
+                    quant_h(i - 3)
+                if i == 3:
+                    mm_0(0)
+                if i % 2 == 1 and i > 1:
+                    quant_dz(i // 2 - 1, H)
+                tanh(i)
+                quant_f(i - 1, R)
+                square(i)
+                f_v(i)
+                z_sum(i + 1, 0)
+                if i == 3:
+                    fin_0(0)
+                quant_f(i - 1, H)
+                if i == 2:
+                    w_quant(Z)
+                z_sig(i + 1, 1)
+                r_pe(i + 1)
+                if i % 2 == 1 and i > 1:
+                    ilvq(i // 2 - 1, R, 1)
+                f_hm(i)
+                f_ndc(i)
+                if i % 2 == 0 and i > 1:
+                    ilvq(i // 2 - 1, Z, 0)
+                if i % 2 == 0 and i > 1:
+                    quant_dz(i // 2 - 1, Z)
+                z_sig(i + 1, 0)
+                if i == 1:
+                    w_transpose(Z, 0)
+                    w_transpose(Z, 1)
+                if i == 3:
+                    mm_0(1)
+                r_sigpe(i + 1)
+                z_back(i + 1, 1)
+                f_dzg(i)
+                alloc_in(i + 2)
+                load(i + 2)
+                if i == 2:
+                    w_transpose(H, 0)
+                    w_transpose(H, 1)
+                if i % 2 == 1 and i > 1:
+                    ilvq(i // 2 - 1, R, 0)
+                if i == 3:
+                    fin_0(1)
+                if i > 2:
+                    mm_0(i - 1)
+                f_dcr(i)
+                if i == 2:
+                    w_quant(H)
+                if i == 2:
+                    w_transpose(R, 0)
+                    w_transpose(R, 1)
+                transpose(i, Z)
+                evac(i, Z)
+                if i % 2 == 0 and i > 1:
+                    ilvq(i // 2 - 1, H, 0)
+                if i > 1:
+                    ilvh(i - 2, 0)
+                if i > 1:
+                    ilvh(i - 2, 1)
+                    if i < 5:
+                        load_h(i - 1)
+                f_drg(i)
+                if i > 2:
+                    fin_0(i - 1)
+                if i % 2 == 1 and i > 1:
+                    quant_dz(i // 2 - 1, R)
+                transpose(i, H)
+                evac(i, H)
+                z_back(i + 1, 0)
+                if i % 2 == 0 and i > 1:
+                    ilvq(i // 2 - 1, H, 1)
+                if i == 2:
+                    w_quant(R)
+                f_gz(i)
+            i = A
+            ilvq(i // 2 - 1, Z, 0)
+            z_sum(i + 1, 1)
+            gate_tile("r", B)
+            gate_tile("q", B)
             dz_tiles(g)
-            mid_tiles(a)
-            f_gq(a)
-            quant_f(a - 1, Z)
-            f_t1(a)
-            quant_f(a - 1, H)
-            f_ac(a)
-            ilv_dz(g - 1, Z)
-            tanh(a)
-            square(a)
-            next_pe(b)
-            quant_f(a - 1, R)
-            f_gz(a)
+            mid_tiles(A)
+            f_t1(A)
+            r_pe(i + 1)
+            f_gq(A)
+            r_v(i + 1)
+            z_sig(i + 1, 1)
+            f_ac(A)
+            transpose(i - 1, R)
+            ilvq(i // 2 - 1, R, 0)
+            quant_f(i - 1, Z)
+            evac(i - 1, R)
+            tanh(A)
+            z_sum(i + 1, 0)
+            f_gz(A)
             quant_h(g)
-            next_v(b)
-            quant_dz(g - 1, Z)
-            ilv_dz(g - 1, H)
-            f_hm(a)
-            mm_0(a - 1)
-            fin_0(a - 1)
-            f_dzg(a)
-            transpose(a, Z)
-            evac(a, Z)
-            ilv_dz(g - 1, R)
-
-            mid_tiles(b)
-            f_gq(b)
-            f_t1(b)
-            quant_dz(g - 1, H)
-            f_ac(b)
-            tanh(b)
-            square(b)
-            f_ndc(a)
-            quant_dz(g - 1, R)
+            quant_f(i - 1, H)
+            mid_tiles(B)
+            quant_f(i - 1, R)
+            r_sigpe(i + 1)
+            z_sig(i + 1, 0)
+            square(A)
+            f_v(A)
+            f_hm(A)
+            f_dzg(A)
+            r_sig(i + 1)
+            mm_0(i - 1)
+            ilvq(i // 2 - 1, Z, 1)
+            z_back(i + 1, 1)
+            f_t1(B)
+            z_back(i + 1, 0)
+            quant_dz(i // 2 - 1, Z)
+            ilvq(i // 2 - 1, H, 0)
+            fin_0(i - 1)
+            transpose(A, Z)
+            ilvq(i // 2 - 1, H, 1)
+            ilvq(i // 2 - 1, R, 1)
+            f_ac(B)
+            tanh(B)
+            quant_dz(i // 2 - 1, R)
+            f_ndc(A)
+            f_gq(B)
+            square(B)
             pass_1(R, range(3), True, True)
-            quant_f(a, Z)
-            f_v(a)
-            f_hm(b)
-            for m in range(4):
-                fin_1(R, m, t["b1", R, m])
+            fin_1(R, 0, t["b1", R, 0])
+            f_hm(B)
+            fin_1(R, 1, t["b1", R, 1])
+            evac(A, Z)
+            fin_1(R, 2, t["b1", R, 2])
+            f_dzg(B)
+            f_ndc(B)
+            f_dcr(A)
+            fin_1(R, 3, t["b1", R, 3])
             pass_1(Z, range(3), True, False)
-            f_dcr(a)
-            f_dzg(b)
-            transpose(b, Z)
-            transpose(a, H)
-            ilv_dz(g, Z)
-            evac(b, Z)
-            evac(a, H)
-            f_ndc(b)
-            f_gz(b)
-            f_dcr(b)
-            transpose(b, H)
+            f_dcr(B)
+            ilvq(g, Z, 0)
+            quant_dz(i // 2 - 1, H)
+            ilvq(g, Z, 1)
+            ilvq(g, H, 0)
+            transpose(A, H)
             quant_dz(g, Z)
+            f_v(B)
+            evac(A, H)
             pass_1(Z, (3,), False, True)
-            quant_f(b, Z)
-            quant_f(a, H)
-            evac(b, H)
-            for m in range(4):
-                fin_1(Z, m, t["b1", Z, m])
-                store_1(Z, m)
+            transpose(B, Z)
+            fin_1(Z, 0, t["b1", Z, 0])
+            store_1(Z, 0)
+            quant_f(A, Z)
+            f_drg(A)
+            fin_1(Z, 1, t["b1", Z, 1])
+            store_1(Z, 1)
+            evac(B, Z)
+            fin_1(Z, 2, t["b1", Z, 2])
+            store_1(Z, 2)
+            quant_f(A, H)
+            ilvq(g, H, 1)
+            quant_f(B, Z)
+            transpose(B, H)
+            transpose(A, R)
+            evac(A, R)
             for j in range(J):
-                mm_0_tile(a, j, (Z, H), True, False)
+                mm_0_tile(A, j, (Z, H), True, False)
+            evac(B, H)
             pass_1(H, range(3), True, False, (0, 1))
-            ilv_dz(g, H)
-            f_v(b)
-            f_drg(a)
-            transpose(a, R)
-            quant_f(b, H)
-            f_drg(b)
-            transpose(b, R)
-            pass_1(H, range(3), True, False, (2, 3))
-            evac(a, R)
-            interleave(nc.scalar.copy, t["dz", g, R], ("ilv", g, R), slice(0, 192))
-            interleave(nc.vector.tensor_copy, t["dz", g, R], ("ilv", g, R), slice(192, C))
-            quant_f(a, R)
-            evac(b, R)
+            f_gz(B)
+            f_drg(B)
+            ilvq(g, R, 0)
+            fin_1(Z, 3, t["b1", Z, 3])
+            store_1(Z, 3)
             quant_dz(g, H)
-            for j in range(J):
-                mm_0_tile(a, j, (R,), False, True)
-            pass_1(H, (3,), False, True)
+            ilvv(g, R, 1)
+            transpose(B, R)
+            pass_1(H, range(3), True, False, (2, 3))
+            evac(B, R)
+            quant_f(A, R)
             quant_dz(g, R)
-            quant_f(b, R)
-            for m in range(4):
-                fin_1(H, m, t["b1", H, m])
-                store_1(H, m)
-            fin_0(a)
-            for m in range(4):
-                pass_1(R, (3,), True, True, (m,), "tr" if m < 2 else "pa")
-                add_1(R, m, t["b1", R, m])
-                store_1(R, m)
-            mm_0(b)
-            fin_0(b)
+            quant_f(B, H)
+            pass_1(H, (3,), False, True)
+            for j in range(J):
+                mm_0_tile(A, j, (R,), False, True)
+            fin_1(H, 0, t["b1", H, 0])
+            store_1(H, 0)
+            quant_f(B, R)
+            fin_1(H, 1, t["b1", H, 1])
+            store_1(H, 1)
+            fin_1(H, 2, t["b1", H, 2])
+            store_1(H, 2)
+            fin_0(A)
+            pass_1(R, (3,), True, True, (2,), "pa")
+            add_1(R, 2, t["b1", R, 2])
+            store_1(R, 2)
+            mm_0(B)
+            for j in range(J):
+                fin_0j(B, j)
+            pass_1(R, (3,), True, True, (0,), "tr")
+            add_1(R, 0, t["b1", R, 0])
+            store_1(R, 0)
+            pass_1(R, (3,), True, True, (1,), "tr")
+            add_1(R, 1, t["b1", R, 1])
+            store_1(R, 1)
+            fin_1(H, 3, t["b1", H, 3])
+            store_1(H, 3)
+            pass_1(R, (3,), True, True, (3,), "pa")
+            add_1(R, 3, t["b1", R, 3])
+            store_1(R, 3)

@@ -179,7 +179,10 @@ def tile_gatedgraphconvolution_pb_v_kernel(
                 t["c2", i] = inp.tile([P, J, C], F32, name="c2", tag="hn")
 
         def f_t1(i, js=ALL):
-            tt(t["t1", i][:, js, :], t["r", i][:, js, :], t["mh", i][:, js, gate(H)], OP.mult)
+            eng = nc.vector if i == 0 else nc.gpsimd
+            eng.tensor_tensor(
+                out=t["t1", i][:, js, :], in0=t["r", i][:, js, :], in1=t["mh", i][:, js, gate(H)], op=OP.mult
+            )
 
         def f_ac(i, js=ALL):
             tt(t["c", i][:, js, :], t["x", i][:, js, gate(H)], t["t1", i][:, js, :], OP.add)
@@ -431,33 +434,33 @@ def tile_gatedgraphconvolution_pb_v_kernel(
             load_hn(2)
             load_h(0)
             i = 0
+            z_sum(i + 1, 1)
+            z_sum(i + 1, 0)
+            f_hm(i)
+            r_pe(i + 1)
+            f_gq(i)
             gate_tile("r", i + 1)
             gate_tile("q", i + 1)
             if i % 2 == 0:
                 dz_tiles(i // 2)
             if i > 0:
                 mid_tiles(i)
-            f_hm(i)
-            f_gq(i)
-            z_sum(i + 1, 0)
-            f_dzg(i)
-            z_sig(i + 1, 0)
-            r_v(i + 1)
-            r_pe(i + 1)
             f_ndc(i)
-            r_sigpe(i + 1)
-            z_sum(i + 1, 1)
+            f_dzg(i)
             z_sig(i + 1, 1)
-            f_gz(i)
-            r_sig(i + 1)
-            f_dcr(i)
             transpose(i, Z)
-            transpose(i, H)
-            evac(i, Z)
-            evac(i, H)
+            f_gz(i)
             z_back(i + 1, 1)
-            z_back(i + 1, 0)
+            f_dcr(i)
+            transpose(i, H)
+            z_sig(i + 1, 0)
+            r_sigpe(i + 1)
+            r_v(i + 1)
+            r_sig(i + 1)
+            evac(i, Z)
             f_drg(i)
+            evac(i, H)
+            z_back(i + 1, 0)
             for i in range(1, CHUNKS - 2):
                 gate_tile("r", i + 1)
                 gate_tile("q", i + 1)
@@ -465,204 +468,213 @@ def tile_gatedgraphconvolution_pb_v_kernel(
                     dz_tiles(i // 2)
                 if i > 0:
                     mid_tiles(i)
-                transpose(i - 1, R)
-                f_t1(i)
-                f_gq(i)
-                evac(i - 1, R)
                 if i % 2 == 0 and i > 1:
                     ilvq(i // 2 - 1, Z, 1)
-                z_sum(i + 1, 1)
-                r_sig(i + 1)
-                f_ac(i)
-                r_v(i + 1)
-                quant_f(i - 1, Z)
-                if i > 2:
-                    quant_h(i - 3)
-                if i == 3:
-                    mm_0(0)
-                if i % 2 == 1 and i > 1:
-                    quant_dz(i // 2 - 1, H)
-                tanh(i)
-                quant_f(i - 1, R)
-                square(i)
-                f_v(i)
-                z_sum(i + 1, 0)
+                transpose(i - 1, R)
                 if i == 3:
                     fin_0(0)
-                quant_f(i - 1, H)
-                if i == 2:
-                    w_quant(Z)
-                z_sig(i + 1, 1)
-                r_pe(i + 1)
-                if i % 2 == 1 and i > 1:
-                    ilvq(i // 2 - 1, R, 1)
-                f_hm(i)
-                f_ndc(i)
-                if i % 2 == 0 and i > 1:
-                    ilvq(i // 2 - 1, Z, 0)
-                if i % 2 == 0 and i > 1:
-                    quant_dz(i // 2 - 1, Z)
-                z_sig(i + 1, 0)
-                if i == 1:
-                    w_transpose(Z, 0)
-                    w_transpose(Z, 1)
-                if i == 3:
-                    mm_0(1)
-                r_sigpe(i + 1)
-                z_back(i + 1, 1)
-                f_dzg(i)
+                if i > 3:
+                    fin_0(i - 2)
+                f_t1(i)
+                f_gq(i)
+                f_ac(i)
                 alloc_in(i + 2)
                 load(i + 2)
-                if i == 2:
-                    w_transpose(H, 0)
-                    w_transpose(H, 1)
+                evac(i - 1, R)
+                if i % 2 == 0 and i > 1:
+                    ilvq(i // 2 - 1, H, 0)
+                tanh(i)
+                quant_f(i - 1, Z)
+                square(i)
                 if i % 2 == 1 and i > 1:
                     ilvq(i // 2 - 1, R, 0)
                 if i == 3:
-                    fin_0(1)
-                if i > 2:
-                    mm_0(i - 1)
-                f_dcr(i)
+                    mm_0(1)
                 if i == 2:
-                    w_quant(H)
+                    w_quant(Z)
                 if i == 2:
                     w_transpose(R, 0)
                     w_transpose(R, 1)
-                transpose(i, Z)
-                evac(i, Z)
+                z_sum(i + 1, 1)
+                if i % 2 == 1 and i > 1:
+                    ilvq(i // 2 - 1, R, 1)
+                f_v(i)
+                if i > 2:
+                    quant_h(i - 3)
+                if i % 2 == 1 and i > 1:
+                    quant_dz(i // 2 - 1, H)
+                z_sig(i + 1, 1)
+                quant_f(i - 1, H)
+                r_pe(i + 1)
                 if i % 2 == 0 and i > 1:
-                    ilvq(i // 2 - 1, H, 0)
+                    ilvq(i // 2 - 1, Z, 0)
+                if i == 1:
+                    w_transpose(Z, 0)
+                    w_transpose(Z, 1)
+                if i == 2:
+                    w_transpose(H, 0)
+                    w_transpose(H, 1)
+                if i == 3:
+                    fin_0(1)
                 if i > 1:
                     ilvh(i - 2, 0)
+                quant_f(i - 1, R)
+                f_hm(i)
+                z_sum(i + 1, 0)
+                r_v(i + 1)
+                f_ndc(i)
+                if i > 2:
+                    mm_0(i - 1)
+                f_dzg(i)
+                r_sig(i + 1)
+                if i % 2 == 0 and i > 1:
+                    quant_dz(i // 2 - 1, Z)
+                z_sig(i + 1, 0)
+                transpose(i, Z)
+                r_sigpe(i + 1)
+                f_dcr(i)
+                if i == 2:
+                    w_quant(R)
+                if i == 2:
+                    w_quant(H)
+                f_drg(i)
                 if i > 1:
                     ilvh(i - 2, 1)
                     if i < 5:
                         load_h(i - 1)
-                f_drg(i)
-                if i > 2:
-                    fin_0(i - 1)
-                if i % 2 == 1 and i > 1:
-                    quant_dz(i // 2 - 1, R)
+                evac(i, Z)
+                if i == 2:
+                    mm_0(0)
                 transpose(i, H)
-                evac(i, H)
-                z_back(i + 1, 0)
                 if i % 2 == 0 and i > 1:
                     ilvq(i // 2 - 1, H, 1)
-                if i == 2:
-                    w_quant(R)
+                evac(i, H)
+                z_back(i + 1, 0)
                 f_gz(i)
+                if i % 2 == 1 and i > 1:
+                    quant_dz(i // 2 - 1, R)
+                z_back(i + 1, 1)
             i = A
-            ilvq(i // 2 - 1, Z, 0)
             z_sum(i + 1, 1)
+            fin_0(i - 2)
             gate_tile("r", B)
             gate_tile("q", B)
             dz_tiles(g)
             mid_tiles(A)
-            f_t1(A)
-            r_pe(i + 1)
-            f_gq(A)
-            r_v(i + 1)
-            z_sig(i + 1, 1)
-            f_ac(A)
-            transpose(i - 1, R)
-            ilvq(i // 2 - 1, R, 0)
-            quant_f(i - 1, Z)
-            evac(i - 1, R)
-            tanh(A)
-            z_sum(i + 1, 0)
-            f_gz(A)
-            quant_h(g)
-            quant_f(i - 1, H)
-            mid_tiles(B)
-            quant_f(i - 1, R)
-            r_sigpe(i + 1)
-            z_sig(i + 1, 0)
-            square(A)
-            f_v(A)
-            f_hm(A)
-            f_dzg(A)
-            r_sig(i + 1)
-            mm_0(i - 1)
             ilvq(i // 2 - 1, Z, 1)
-            z_back(i + 1, 1)
-            f_t1(B)
-            z_back(i + 1, 0)
-            quant_dz(i // 2 - 1, Z)
-            ilvq(i // 2 - 1, H, 0)
-            fin_0(i - 1)
-            transpose(A, Z)
-            ilvq(i // 2 - 1, H, 1)
+            f_gq(A)
+            z_sig(i + 1, 1)
+            r_v(i + 1)
+            transpose(i - 1, R)
+            f_t1(A)
+            quant_h(g)
+            f_ac(A)
+            r_pe(i + 1)
             ilvq(i // 2 - 1, R, 1)
-            f_ac(B)
-            tanh(B)
+            ilvq(i // 2 - 1, R, 0)
+            f_gz(A)
             quant_dz(i // 2 - 1, R)
-            f_ndc(A)
+            evac(i - 1, R)
+            quant_f(i - 1, Z)
+            tanh(A)
+            z_back(i + 1, 1)
+            quant_f(i - 1, R)
+            z_sum(i + 1, 0)
+            square(A)
+            r_sig(i + 1)
+            z_sig(i + 1, 0)
+            mid_tiles(B)
+            r_sigpe(i + 1)
+            quant_f(i - 1, H)
+            ilvq(i // 2 - 1, H, 0)
+            ilvq(i // 2 - 1, Z, 0)
+            f_hm(A)
+            z_back(i + 1, 0)
+            f_t1(B)
+            f_dzg(A)
             f_gq(B)
+            mm_0(i - 1)
+            ilvq(i // 2 - 1, H, 1)
+            f_ac(B)
+            f_ndc(A)
+            f_v(A)
+            transpose(A, Z)
+            tanh(B)
+            fin_0(B - 2)
             square(B)
+            f_hm(B)
             pass_1(R, range(3), True, True)
             fin_1(R, 0, t["b1", R, 0])
-            f_hm(B)
-            fin_1(R, 1, t["b1", R, 1])
-            evac(A, Z)
+            quant_dz(i // 2 - 1, Z)
             fin_1(R, 2, t["b1", R, 2])
+            evac(A, Z)
             f_dzg(B)
-            f_ndc(B)
-            f_dcr(A)
             fin_1(R, 3, t["b1", R, 3])
+            fin_1(R, 1, t["b1", R, 1])
+            f_ndc(B)
             pass_1(Z, range(3), True, False)
-            f_dcr(B)
-            ilvq(g, Z, 0)
-            quant_dz(i // 2 - 1, H)
+            f_dcr(A)
+            transpose(B, Z)
             ilvq(g, Z, 1)
-            ilvq(g, H, 0)
+            f_dcr(B)
             transpose(A, H)
+            ilvq(g, Z, 0)
             quant_dz(g, Z)
             f_v(B)
-            evac(A, H)
+            quant_dz(i // 2 - 1, H)
+            f_drg(A)
             pass_1(Z, (3,), False, True)
-            transpose(B, Z)
+            f_drg(B)
+            evac(B, Z)
+            transpose(B, H)
+            evac(A, H)
+            quant_f(A, Z)
+            ilvq(g, H, 0)
             fin_1(Z, 0, t["b1", Z, 0])
             store_1(Z, 0)
-            quant_f(A, Z)
-            f_drg(A)
             fin_1(Z, 1, t["b1", Z, 1])
             store_1(Z, 1)
-            evac(B, Z)
+            pass_1(H, range(3), True, False, (0, 1))
             fin_1(Z, 2, t["b1", Z, 2])
             store_1(Z, 2)
-            quant_f(A, H)
-            ilvq(g, H, 1)
-            quant_f(B, Z)
-            transpose(B, H)
-            transpose(A, R)
-            evac(A, R)
-            for j in range(J):
-                mm_0_tile(A, j, (Z, H), True, False)
+            ilvv(g, R, 1)
             evac(B, H)
-            pass_1(H, range(3), True, False, (0, 1))
-            f_gz(B)
-            f_drg(B)
-            ilvq(g, R, 0)
+            ilvq(g, H, 1)
+            transpose(A, R)
+            transpose(B, R)
+            evac(A, R)
+            quant_dz(g, H)
             fin_1(Z, 3, t["b1", Z, 3])
             store_1(Z, 3)
-            quant_dz(g, H)
-            ilvv(g, R, 1)
-            transpose(B, R)
+            quant_f(B, Z)
+            f_gz(B)
+            ilvq(g, R, 0)
             pass_1(H, range(3), True, False, (2, 3))
             evac(B, R)
-            quant_f(A, R)
             quant_dz(g, R)
-            quant_f(B, H)
+            quant_f(A, R)
+            quant_f(A, H)
             pass_1(H, (3,), False, True)
-            for j in range(J):
-                mm_0_tile(A, j, (R,), False, True)
+            quant_f(B, R)
             fin_1(H, 0, t["b1", H, 0])
             store_1(H, 0)
-            quant_f(B, R)
             fin_1(H, 1, t["b1", H, 1])
             store_1(H, 1)
+            fin_1(H, 3, t["b1", H, 3])
+            store_1(H, 3)
             fin_1(H, 2, t["b1", H, 2])
             store_1(H, 2)
+            quant_f(B, H)
+            pass_1(R, (3,), True, True, (1,), "tr")
+            add_1(R, 1, t["b1", R, 1])
+            store_1(R, 1)
+            pass_1(R, (3,), True, True, (0,), "tr")
+            add_1(R, 0, t["b1", R, 0])
+            store_1(R, 0)
+            for j in range(J):
+                mm_0_tile(A, j, (Z, H), True, False)
+            for j in range(J):
+                mm_0_tile(A, j, (R,), False, True)
             fin_0(A)
             pass_1(R, (3,), True, True, (2,), "pa")
             add_1(R, 2, t["b1", R, 2])
@@ -670,14 +682,6 @@ def tile_gatedgraphconvolution_pb_v_kernel(
             mm_0(B)
             for j in range(J):
                 fin_0j(B, j)
-            pass_1(R, (3,), True, True, (0,), "tr")
-            add_1(R, 0, t["b1", R, 0])
-            store_1(R, 0)
-            pass_1(R, (3,), True, True, (1,), "tr")
-            add_1(R, 1, t["b1", R, 1])
-            store_1(R, 1)
-            fin_1(H, 3, t["b1", H, 3])
-            store_1(H, 3)
             pass_1(R, (3,), True, True, (3,), "pa")
             add_1(R, 3, t["b1", R, 3])
             store_1(R, 3)

@@ -178,8 +178,7 @@ def tile_gatedgraphconvolution_pb_v_kernel(
                 t["gq", i] = inp.tile([P, J, C], F32, name="gq", tag="x")
                 t["c2", i] = inp.tile([P, J, C], F32, name="c2", tag="hn")
 
-        def f_t1(i, js=ALL):
-            eng = nc.vector if i == 0 else nc.gpsimd
+        def f_t1(i, js=ALL, eng=nc.vector):
             eng.tensor_tensor(
                 out=t["t1", i][:, js, :], in0=t["r", i][:, js, :], in1=t["mh", i][:, js, gate(H)], op=OP.mult
             )
@@ -244,15 +243,26 @@ def tile_gatedgraphconvolution_pb_v_kernel(
                     nc.tensor.transpose(bank[:, u, j * P : (j + 1) * P], words[:, u : C // 2 : 2], id_f[:])
 
         def evac(i, q):
-            t["dzT", i, q] = mx.tile([P, 2 * P, 4], BF16, name="dzT", tag="dzT", bufs=4, align_bytes=64)
-            nc.scalar.copy(out=t["dzT", i, q][:].bitcast(F32), in_=t["tr", i, q][:].rearrange("p u r -> p r u"))
+            if q == H:
+                t["dzT", i, H] = mx.tile([P, 1, 2 * P, 4], BF16, name="dzTh", tag="dzTh", bufs=2, align_bytes=64)
+            elif ("dzT", i, Z) not in t:
+                t["dzT", i, Z] = mx.tile([P, 2, 2 * P, 4], BF16, name="dzTp", tag="wide", bufs=4, align_bytes=64)
+                t["dzT", i, R] = t["dzT", i, Z]
+            k = 1 if q == R else 0
+            nc.scalar.copy(
+                out=t["dzT", i, q][:, k, :, :].bitcast(F32), in_=t["tr", i, q][:].rearrange("p u r -> p r u")
+            )
 
-        def quant_f(i, q):
-            codes = mx.tile([P, 2 * P], U32, name="f_codes", tag="f_codes", bufs=9, align_bytes=64)
-            scales = mx.tile([P, 2 * P], U8, name="f_scales", tag="f_scales", bufs=9, align_bytes=64)
-            t["fc", i, q], t["fs", i, q] = codes, scales
+        def quant_f(i, gates):
+            n = len(gates)
+            codes = mx.tile([P, n, 2 * P], U32, name="f_codes", tag="f_codes%d" % n, bufs=3, align_bytes=64)
+            scales = mx.tile([P, n, 2 * P], U8, name="f_scales", tag="f_scales%d" % n, bufs=3, align_bytes=64)
+            for k, q in enumerate(gates):
+                t["fc", i, q], t["fs", i, q] = codes[:, k, :], scales[:, k, :]
             nc.vector.quantize_mx(
-                out=codes[:].bitcast(E5X4), scales=scales[:], in_=t["dzT", i, q][:].rearrange("p r t -> p (r t)")
+                out=codes[:].rearrange("p n r -> p (n r)").bitcast(E5X4),
+                scales=scales[:].rearrange("p n r -> p (n r)"),
+                in_=t["dzT", i, gates[0]][:].rearrange("p n r t -> p (n r t)"),
             )
 
         def mm_0_tile(i, j, gates, first, last):
@@ -272,7 +282,7 @@ def tile_gatedgraphconvolution_pb_v_kernel(
 
         def mm_0(i):
             for j in range(J):
-                mm_0_tile(i, j, (Z, H, R), True, True)
+                mm_0_tile(i, j, (Z, R, H), True, True)
 
         def fin_0(i):
             g, js = rows(i)
@@ -344,7 +354,7 @@ def tile_gatedgraphconvolution_pb_v_kernel(
                 for u in range(2):
                     nc.tensor.transpose(bank[:, u, b * P : (b + 1) * P], words[:, u : C // 2 : 2], id_f[:])
             if half == 0:
-                t["wT", q] = mx.tile([P, C, 4], BF16, name="wT", tag="wT", bufs=3, align_bytes=64)
+                t["wT", q] = mx.tile([P, C, 4], BF16, name="wT", tag="wide", bufs=4, align_bytes=64)
             nc.scalar.copy(
                 out=t["wT", q][:, half * 2 * P : (half + 1) * 2 * P, :].bitcast(F32),
                 in_=bank[:].rearrange("p u r -> p r u"),
@@ -434,254 +444,252 @@ def tile_gatedgraphconvolution_pb_v_kernel(
             load_hn(2)
             load_h(0)
             i = 0
-            z_sum(i + 1, 1)
-            z_sum(i + 1, 0)
             f_hm(i)
-            r_pe(i + 1)
-            f_gq(i)
+            z_sum(i + 1, 0)
             gate_tile("r", i + 1)
             gate_tile("q", i + 1)
             if i % 2 == 0:
                 dz_tiles(i // 2)
             if i > 0:
                 mid_tiles(i)
-            f_ndc(i)
+            f_gq(i)
+            z_sum(i + 1, 1)
             f_dzg(i)
-            z_sig(i + 1, 1)
-            transpose(i, Z)
-            f_gz(i)
-            z_back(i + 1, 1)
-            f_dcr(i)
-            transpose(i, H)
+            f_ndc(i)
             z_sig(i + 1, 0)
-            r_sigpe(i + 1)
+            r_pe(i + 1)
             r_v(i + 1)
-            r_sig(i + 1)
-            evac(i, Z)
             f_drg(i)
-            evac(i, H)
+            r_sig(i + 1)
+            z_sig(i + 1, 1)
             z_back(i + 1, 0)
+            transpose(i, R)
+            r_sigpe(i + 1)
+            transpose(i, Z)
+            evac(i, R)
+            f_gz(i)
+            f_dcr(i)
+            z_back(i + 1, 1)
+            evac(i, Z)
             for i in range(1, CHUNKS - 2):
+                transpose(i - 1, H)
+                if i % 2 == 0 and i > 1:
+                    ilvq(i // 2 - 1, Z, 0)
+                if i == 3:
+                    fin_0(0)
+                if i > 3:
+                    fin_0(i - 2)
                 gate_tile("r", i + 1)
                 gate_tile("q", i + 1)
                 if i % 2 == 0:
                     dz_tiles(i // 2)
                 if i > 0:
                     mid_tiles(i)
-                if i % 2 == 0 and i > 1:
-                    ilvq(i // 2 - 1, Z, 1)
-                transpose(i - 1, R)
-                if i == 3:
-                    fin_0(0)
-                if i > 3:
-                    fin_0(i - 2)
-                f_t1(i)
-                f_gq(i)
-                f_ac(i)
-                alloc_in(i + 2)
-                load(i + 2)
-                evac(i - 1, R)
-                if i % 2 == 0 and i > 1:
-                    ilvq(i // 2 - 1, H, 0)
-                tanh(i)
-                quant_f(i - 1, Z)
-                square(i)
                 if i % 2 == 1 and i > 1:
                     ilvq(i // 2 - 1, R, 0)
+                if i < 3:
+                    f_t1(i, 1)
+                if i % 2 == 0 and i > 1:
+                    ilvq(i // 2 - 1, H, 0)
+                f_gq(i)
+                f_t1(i, ALL if i > 2 else 0, nc.gpsimd)
                 if i == 3:
                     mm_0(1)
-                if i == 2:
-                    w_quant(Z)
-                if i == 2:
-                    w_transpose(R, 0)
-                    w_transpose(R, 1)
-                z_sum(i + 1, 1)
-                if i % 2 == 1 and i > 1:
-                    ilvq(i // 2 - 1, R, 1)
-                f_v(i)
                 if i > 2:
                     quant_h(i - 3)
+                if i % 2 == 0 and i > 1:
+                    ilvq(i // 2 - 1, Z, 1)
+                z_sum(i + 1, 0)
+                f_ac(i)
+                evac(i - 1, H)
+                tanh(i)
+                r_pe(i + 1)
+                square(i)
+                z_sig(i + 1, 0)
+                if i % 2 == 0 and i > 1:
+                    quant_dz(i // 2 - 1, Z)
                 if i % 2 == 1 and i > 1:
                     quant_dz(i // 2 - 1, H)
-                z_sig(i + 1, 1)
-                quant_f(i - 1, H)
-                r_pe(i + 1)
-                if i % 2 == 0 and i > 1:
-                    ilvq(i // 2 - 1, Z, 0)
+                if i == 3:
+                    fin_0(1)
+                if i % 2 == 1 and i > 1:
+                    ilvq(i // 2 - 1, R, 1)
+                alloc_in(i + 2)
+                load(i + 2)
+                if i == 2:
+                    w_quant(Z)
                 if i == 1:
                     w_transpose(Z, 0)
                     w_transpose(Z, 1)
-                if i == 2:
-                    w_transpose(H, 0)
-                    w_transpose(H, 1)
-                if i == 3:
-                    fin_0(1)
-                if i > 1:
-                    ilvh(i - 2, 0)
-                quant_f(i - 1, R)
-                f_hm(i)
-                z_sum(i + 1, 0)
                 r_v(i + 1)
+                f_v(i)
+                quant_f(i - 1, (H,))
+                if i == 2:
+                    w_transpose(R, 0)
+                    w_transpose(R, 1)
+                quant_f(i - 1, (Z, R))
+                z_sum(i + 1, 1)
+                f_hm(i)
                 f_ndc(i)
+                if i == 2:
+                    w_quant(R)
                 if i > 2:
                     mm_0(i - 1)
                 f_dzg(i)
+                f_drg(i)
+                if i > 1:
+                    ilvh(i - 2, 0)
                 r_sig(i + 1)
-                if i % 2 == 0 and i > 1:
-                    quant_dz(i // 2 - 1, Z)
-                z_sig(i + 1, 0)
-                transpose(i, Z)
-                r_sigpe(i + 1)
-                f_dcr(i)
                 if i == 2:
-                    w_quant(R)
+                    w_transpose(H, 0)
+                    w_transpose(H, 1)
+                z_back(i + 1, 0)
+                transpose(i, Z)
                 if i == 2:
                     w_quant(H)
-                f_drg(i)
+                if i == 2:
+                    mm_0(0)
+                z_sig(i + 1, 1)
                 if i > 1:
                     ilvh(i - 2, 1)
                     if i < 5:
                         load_h(i - 1)
                 evac(i, Z)
-                if i == 2:
-                    mm_0(0)
-                transpose(i, H)
-                if i % 2 == 0 and i > 1:
-                    ilvq(i // 2 - 1, H, 1)
-                evac(i, H)
-                z_back(i + 1, 0)
-                f_gz(i)
                 if i % 2 == 1 and i > 1:
                     quant_dz(i // 2 - 1, R)
+                f_dcr(i)
+                r_sigpe(i + 1)
+                f_gz(i)
+                transpose(i, R)
+                evac(i, R)
                 z_back(i + 1, 1)
+                if i % 2 == 0 and i > 1:
+                    ilvq(i // 2 - 1, H, 1)
             i = A
             z_sum(i + 1, 1)
+            z_sum(i + 1, 0)
+            ilvq(i // 2 - 1, R, 0)
+            ilvq(i // 2 - 1, R, 1)
             fin_0(i - 2)
             gate_tile("r", B)
             gate_tile("q", B)
             dz_tiles(g)
             mid_tiles(A)
-            ilvq(i // 2 - 1, Z, 1)
+            f_t1(A, ALL, nc.gpsimd)
+            z_sig(i + 1, 0)
             f_gq(A)
+            r_pe(i + 1)
+            transpose(i - 1, H)
+            f_ac(A)
             z_sig(i + 1, 1)
             r_v(i + 1)
-            transpose(i - 1, R)
-            f_t1(A)
-            quant_h(g)
-            f_ac(A)
-            r_pe(i + 1)
-            ilvq(i // 2 - 1, R, 1)
-            ilvq(i // 2 - 1, R, 0)
-            f_gz(A)
-            quant_dz(i // 2 - 1, R)
-            evac(i - 1, R)
-            quant_f(i - 1, Z)
             tanh(A)
-            z_back(i + 1, 1)
-            quant_f(i - 1, R)
-            z_sum(i + 1, 0)
-            square(A)
-            r_sig(i + 1)
-            z_sig(i + 1, 0)
             mid_tiles(B)
-            r_sigpe(i + 1)
-            quant_f(i - 1, H)
-            ilvq(i // 2 - 1, H, 0)
-            ilvq(i // 2 - 1, Z, 0)
-            f_hm(A)
+            r_sig(i + 1)
+            quant_h(g)
+            f_gz(A)
+            z_back(i + 1, 1)
             z_back(i + 1, 0)
-            f_t1(B)
-            f_dzg(A)
-            f_gq(B)
-            mm_0(i - 1)
+            quant_dz(i // 2 - 1, R)
+            quant_f(i - 1, (Z, R))
+            square(A)
+            r_sigpe(i + 1)
+            f_hm(A)
+            f_t1(B, ALL, nc.gpsimd)
+            ilvq(i // 2 - 1, Z, 1)
+            ilvq(i // 2 - 1, H, 0)
             ilvq(i // 2 - 1, H, 1)
+            f_gq(B)
+            f_dzg(A)
             f_ac(B)
-            f_ndc(A)
-            f_v(A)
-            transpose(A, Z)
+            evac(i - 1, H)
+            quant_f(i - 1, (H,))
             tanh(B)
-            fin_0(B - 2)
-            square(B)
-            f_hm(B)
             pass_1(R, range(3), True, True)
+            square(B)
+            mm_0(i - 1)
+            f_ndc(A)
+            ilvq(i // 2 - 1, Z, 0)
             fin_1(R, 0, t["b1", R, 0])
-            quant_dz(i // 2 - 1, Z)
             fin_1(R, 2, t["b1", R, 2])
-            evac(A, Z)
-            f_dzg(B)
-            fin_1(R, 3, t["b1", R, 3])
+            fin_0(B - 2)
             fin_1(R, 1, t["b1", R, 1])
+            transpose(A, Z)
+            f_hm(B)
+            quant_dz(i // 2 - 1, Z)
+            fin_1(R, 3, t["b1", R, 3])
+            f_dzg(B)
+            evac(A, Z)
             f_ndc(B)
-            pass_1(Z, range(3), True, False)
             f_dcr(A)
-            transpose(B, Z)
             ilvq(g, Z, 1)
             f_dcr(B)
-            transpose(A, H)
             ilvq(g, Z, 0)
+            pass_1(Z, range(3), True, False)
             quant_dz(g, Z)
+            transpose(B, Z)
+            f_v(A)
+            ilvq(g, H, 1)
+            pass_1(Z, (3,), False, True)
+            evac(B, Z)
             f_v(B)
             quant_dz(i // 2 - 1, H)
-            f_drg(A)
-            pass_1(Z, (3,), False, True)
-            f_drg(B)
-            evac(B, Z)
+            transpose(A, H)
             transpose(B, H)
-            evac(A, H)
-            quant_f(A, Z)
-            ilvq(g, H, 0)
             fin_1(Z, 0, t["b1", Z, 0])
             store_1(Z, 0)
-            fin_1(Z, 1, t["b1", Z, 1])
-            store_1(Z, 1)
-            pass_1(H, range(3), True, False, (0, 1))
-            fin_1(Z, 2, t["b1", Z, 2])
-            store_1(Z, 2)
-            ilvv(g, R, 1)
-            evac(B, H)
-            ilvq(g, H, 1)
-            transpose(A, R)
-            transpose(B, R)
-            evac(A, R)
-            quant_dz(g, H)
             fin_1(Z, 3, t["b1", Z, 3])
             store_1(Z, 3)
-            quant_f(B, Z)
+            fin_1(Z, 2, t["b1", Z, 2])
+            store_1(Z, 2)
+            fin_1(Z, 1, t["b1", Z, 1])
+            store_1(Z, 1)
+            evac(B, H)
+            evac(A, H)
+            f_drg(B)
+            f_drg(A)
+            pass_1(H, range(3), True, False, (0, 1))
             f_gz(B)
-            ilvq(g, R, 0)
+            ilvq(g, H, 0)
             pass_1(H, range(3), True, False, (2, 3))
-            evac(B, R)
-            quant_dz(g, R)
-            quant_f(A, R)
-            quant_f(A, H)
+            quant_dz(g, H)
+            ilvv(g, R, 1)
+            transpose(A, R)
+            ilvq(g, R, 0)
+            evac(A, R)
             pass_1(H, (3,), False, True)
-            quant_f(B, R)
+            quant_f(A, (H,))
             fin_1(H, 0, t["b1", H, 0])
             store_1(H, 0)
+            quant_dz(g, R)
+            quant_f(B, (H,))
+            quant_f(A, (Z, R))
+            fin_1(H, 2, t["b1", H, 2])
+            store_1(H, 2)
+            transpose(B, R)
+            evac(B, R)
+            pass_1(R, (3,), True, True, (3,), "pa")
+            add_1(R, 3, t["b1", R, 3])
+            store_1(R, 3)
             fin_1(H, 1, t["b1", H, 1])
             store_1(H, 1)
             fin_1(H, 3, t["b1", H, 3])
             store_1(H, 3)
-            fin_1(H, 2, t["b1", H, 2])
-            store_1(H, 2)
-            quant_f(B, H)
+            for j in range(J):
+                mm_0_tile(A, j, (H,), True, False)
+            for j in range(J):
+                mm_0_tile(A, j, (Z, R), False, True)
+            quant_f(B, (Z, R))
+            fin_0(A)
             pass_1(R, (3,), True, True, (1,), "tr")
             add_1(R, 1, t["b1", R, 1])
             store_1(R, 1)
             pass_1(R, (3,), True, True, (0,), "tr")
             add_1(R, 0, t["b1", R, 0])
             store_1(R, 0)
-            for j in range(J):
-                mm_0_tile(A, j, (Z, H), True, False)
-            for j in range(J):
-                mm_0_tile(A, j, (R,), False, True)
-            fin_0(A)
-            pass_1(R, (3,), True, True, (2,), "pa")
-            add_1(R, 2, t["b1", R, 2])
-            store_1(R, 2)
             mm_0(B)
             for j in range(J):
                 fin_0j(B, j)
-            pass_1(R, (3,), True, True, (3,), "pa")
-            add_1(R, 3, t["b1", R, 3])
-            store_1(R, 3)
+            pass_1(R, (3,), True, True, (2,), "pa")
+            add_1(R, 2, t["b1", R, 2])
+            store_1(R, 2)

@@ -298,7 +298,10 @@ def tile_gatedgraphconvolution_pb_v_kernel(
         def interleave(copy, src, key, cols=slice(0, C)):
             if key not in t:
                 t[key] = mx.tile([P, C, 4], BF16, name="ilv", tag="ilv", bufs=3, align_bytes=64)
-            copy(out=t[key][:, cols, :], in_=src[:, :, cols].rearrange("p j w -> p w j"))
+            copy(
+                out=t[key][:, cols, :].rearrange("p (c i) t -> p c t i", i=4),
+                in_=src[:, :, cols].rearrange("p t (c i) -> p c t i", i=4),
+            )
 
         def quant_t(key, codes, scales, dt):
             nc.vector.quantize_mx(

from contextlib import ExitStack

import concourse.mybir as mybir
from concourse.masks import make_identity

TOKENS, C, G = 2048, 512, 1536
FLOPS = 2 * 2 * TOKENS * C * G
BYTES = TOKENS * G * 6 + TOKENS * C * 8 + C * G * 2 + TOKENS * C * 4 + C * G * 4

F32 = mybir.dt.float32
BF16 = mybir.dt.bfloat16
U32 = mybir.dt.uint32
U8 = mybir.dt.uint8
E4X4 = mybir.dt.float8_e4m3fn_x4
E5X4 = mybir.dt.float8_e5m2_x4
ACT = mybir.ActivationFunctionType
OP = mybir.AluOpType

P = 128
GROUPS = 4
CHUNKS = 8
J = 2
Z, R, H = 0, 1, 2


def gate(q):
    return slice(q * C, (q + 1) * C)


def tile_gatedgraphconvolution_pb_v_kernel(
    tc, x_proj, annotations, recurrent_kernel, bias_h, mh, h_new, grad_out, out_0, out_1
):
    nc = tc.nc
    x_v = x_proj.rearrange("(g p j) w -> g p j w", g=GROUPS, j=4)
    mh_v = mh.rearrange("(g p j) w -> g p j w", g=GROUPS, j=4)
    hn_v = h_new.rearrange("g (p j) w -> g p j w", j=4)
    g_v = grad_out.rearrange("g (p j) w -> g p j w", j=4)
    h_v = annotations.rearrange("g (p j) w -> g p j w", j=4)
    o_v = out_0.rearrange("g (p j) w -> g p j w", j=4)
    w_v = recurrent_kernel.rearrange("(b p) w -> p b w", p=P)

    with ExitStack() as ctx:
        keep = ctx.enter_context(tc.tile_pool(name="keep", bufs=1))
        inp = ctx.enter_context(tc.tile_pool(name="inp", bufs=3))
        mid = ctx.enter_context(tc.tile_pool(name="mid", bufs=1))
        mx = ctx.enter_context(tc.tile_pool(name="mx", bufs=2))
        psum = ctx.enter_context(tc.psum_pool(name="psum", bufs=2))

        id_f = keep.tile([P, P], F32, name="id_f")
        id_b = keep.tile([P, P], BF16, name="id_b")
        warm = keep.tile([P, 1], F32, name="warm")
        make_identity(nc, id_f[:])
        make_identity(nc, id_b[:])
        nc.vector.memset(warm[:], 0.0)
        nc.scalar.activation(out=warm[:], in_=warm[:], func=ACT.Sigmoid)

        w_codes, w_scales, tok_codes, tok_scales, h_codes, h_scales = {}, {}, {}, {}, {}, {}
        for q in range(3):
            w_codes[q] = keep.tile([P, C], U32, name="w_codes%d" % q, align_bytes=64)
            w_scales[q] = keep.tile([P, C], U8, name="w_scales%d" % q, align_bytes=64)
        for g in range(GROUPS):
            h_codes[g] = keep.tile([P, C], U32, name="h_codes%d" % g, align_bytes=64)
            h_scales[g] = keep.tile([P, C], U8, name="h_scales%d" % g, align_bytes=64)
            for q in range(3):
                tok_codes[g, q] = keep.tile([P, C], U32, name="tok_codes%d_%d" % (g, q), align_bytes=64)
                tok_scales[g, q] = keep.tile([P, C], U8, name="tok_scales%d_%d" % (g, q), align_bytes=64)

        t = {}

        def alloc_in(i):
            t["x", i] = inp.tile([P, J, G], BF16, name="x", tag="x")
            t["mh", i] = inp.tile([P, J, G], F32, name="mh", tag="mh")
            t["g", i] = inp.tile([P, J, C], BF16, name="gin", tag="g")
            t["hn", i] = inp.tile([P, J, C], F32, name="hn", tag="hn")

        def rows(i):
            return i // 2, slice((i % 2) * J, (i % 2) * J + J)

        def load(i):
            g, js = rows(i)
            nc.sync.dma_start(out=t["mh", i][:], in_=mh_v[g][:, js, :])
            nc.sync.dma_start(out=t["x", i][:], in_=x_v[g][:, js, :])
            nc.sync.dma_start(out=t["g", i][:], in_=g_v[g][:, js, :])
            nc.sync.dma_start(out=t["hn", i][:], in_=hn_v[g][:, js, :])

        def load_first():
            for j in range(J):
                nc.sync.dma_start(out=t["mh", 0][:, j, gate(R)], in_=mh_v[0][:, j, gate(R)])
                nc.sync.dma_start(out=t["x", 0][:, j, gate(R)], in_=x_v[0][:, j, gate(R)])
            for q in (H, Z):
                nc.sync.dma_start(out=t["mh", 0][:, :, gate(q)], in_=mh_v[0][:, 0:J, gate(q)])
                nc.sync.dma_start(out=t["x", 0][:, :, gate(q)], in_=x_v[0][:, 0:J, gate(q)])
            nc.sync.dma_start(out=t["hn", 0][:], in_=hn_v[0][:, 0:J, :])
            nc.sync.dma_start(out=t["g", 0][:], in_=g_v[0][:, 0:J, :])

        def load_gates(i, gates):
            g, js = rows(i)
            for q in gates:
                nc.sync.dma_start(out=t["mh", i][:, :, gate(q)], in_=mh_v[g][:, js, gate(q)])
                nc.sync.dma_start(out=t["x", i][:, :, gate(q)], in_=x_v[g][:, js, gate(q)])

        def load_g(i):
            g, js = rows(i)
            nc.sync.dma_start(out=t["g", i][:], in_=g_v[g][:, js, :])

        def load_hn(i):
            g, js = rows(i)
            nc.sync.dma_start(out=t["hn", i][:], in_=hn_v[g][:, js, :])

        def load_h(g):
            t["h", g] = inp.tile([P, 4, C], BF16, name="h", tag="h", bufs=1)
            nc.sync.dma_start(out=t["h", g][:], in_=h_v[g])

        def tt(out, a, b, op):
            nc.vector.tensor_tensor(out=out, in0=a, in1=b, op=op)

        def stt(out, a, s, b, op0, op1):
            nc.vector.scalar_tensor_tensor(out=out, in0=a, scalar=s, in1=b, op0=op0, op1=op1)

        ALL = slice(0, J)

        def gate_tile(k, i):
            t[k, i] = mid.tile([P, J, C], F32, name=k, tag=k, bufs=2)

        def pe_add(k, q, i, j):
            bank = psum.tile([P, C], F32, name="pa", tag="pa", bufs=4)
            t["pa", k, i, j] = bank
            nc.tensor.matmul(bank[:], lhsT=id_b[:], rhs=t["x", i][:, j, gate(q)], start=True, stop=False)
            nc.tensor.matmul(bank[:], lhsT=id_f[:], rhs=t["mh", i][:, j, gate(q)], start=False, stop=True)

        def z_sum(i, j):
            bank = psum.tile([P, 4, P], F32, name="pa", tag="pa", bufs=4)
            t["z1", i, j] = bank
            for b in range(4):
                cols = slice(b * P, (b + 1) * P)
                nc.tensor.matmul(
                    bank[:, b, :], lhsT=t["mh", i][:, j, cols], rhs=id_f[:], start=(b == 0), stop=False, is_transpose=True
                )
            for b in range(4):
                cols = slice(b * P, (b + 1) * P)
                nc.tensor.matmul(bank[:, b, :], lhsT=t["x", i][:, j, cols], rhs=id_b[:], start=False, stop=(b == 3))

        def z_sig(i, j):
            nc.scalar.activation(
                out=t["q", i][:, j, :],
                in_=t["z1", i, j][:].rearrange("p b k -> p (b k)"),
                func=ACT.Sigmoid,
                scale=-1.0,
            )

        def z_back(i, j):
            bank = psum.tile([P, 4, P], F32, name="pa", tag="pa", bufs=4)
            t["z2", i, j] = bank
            for b in range(4):
                nc.tensor.transpose(bank[:, b, :], t["q", i][:, j, b * P : (b + 1) * P], id_f[:])

        def v_add(k, q, i, js=ALL):
            tt(t[k, i][:, js, :], t["x", i][:, js, gate(q)], t["mh", i][:, js, gate(q)], OP.add)

        def sig(k, i, js=ALL):
            nc.scalar.activation(
                out=t[k, i][:, js, :], in_=t[k, i][:, js, :], func=ACT.Sigmoid, scale=-1.0 if k == "q" else 1.0
            )

        def sig_pe(k, i, j):
            nc.scalar.activation(
                out=t[k, i][:, j, :], in_=t["pa", k, i, j][:], func=ACT.Sigmoid, scale=-1.0 if k == "q" else 1.0
            )

        def mid_tiles(i):
            t["c", i] = mid.tile([P, J, C], F32, name="c", tag="c")
            if i < CHUNKS - 1:
                t["t1", i] = mid.tile([P, J, C], F32, name="t1", tag="t1")
                t["gq", i] = mid.tile([P, J, C], F32, name="gq", tag="gq")
                t["c2", i] = mid.tile([P, J, C], F32, name="c2", tag="c2")
            else:
                t["t1", i] = inp.tile([P, J, C], F32, name="t1", tag="hn")
                t["gq", i] = inp.tile([P, J, C], F32, name="gq", tag="x")
                t["c2", i] = inp.tile([P, J, C], F32, name="c2", tag="hn")

        def f_t1(i, js=ALL, eng=nc.vector):
            eng.tensor_tensor(
                out=t["t1", i][:, js, :], in0=t["r", i][:, js, :], in1=t["mh", i][:, js, gate(H)], op=OP.mult
            )

        def f_ac(i, js=ALL):
            tt(t["c", i][:, js, :], t["x", i][:, js, gate(H)], t["t1", i][:, js, :], OP.add)

        def f_gq(i, js=ALL):
            if ("z2", i, 0) in t:
                for j in range(J):
                    tt(
                        t["gq", i][:, j, :],
                        t["z2", i, j][:].rearrange("p b k -> p (b k)"),
                        t["g", i][:, j, :],
                        OP.mult,
                    )
                return
            tt(t["gq", i][:, js, :], t["g", i][:, js, :], t["q", i][:, js, :], OP.mult)

        def f_gz(i):
            t["gz", i] = mid.tile([P, J, C], F32, name="gz", tag="gz", bufs=3)
            tt(t["gz", i][:], t["g", i][:], t["gq", i][:], OP.subtract)

        def f_v(i):
            stt(t["t1", i][:], t["r", i][:], 1.0, t["t1", i][:], OP.subtract, OP.mult)

        def tanh(i, js=ALL):
            nc.scalar.activation(out=t["c", i][:, js, :], in_=t["c", i][:, js, :], func=ACT.Tanh)

        def square(i, js=ALL):
            nc.scalar.activation(out=t["c2", i][:, js, :], in_=t["c", i][:, js, :], func=ACT.Square)

        def f_hm(i):
            tt(t["c", i][:], t["hn", i][:], t["c", i][:], OP.subtract)

        def dz_tiles(g):
            for q in range(3):
                t["dz", g, q] = mx.tile([P, 4, C], BF16, name="dz%d" % q, tag="dz%d" % q)

        def f_ndc(i):
            stt(t["c2", i][:], t["c2", i][:], 1.0, t["gq", i][:], OP.subtract, OP.mult)

        def f_dzg(i):
            g, js = rows(i)
            tt(t["dz", g, Z][:, js, :], t["c", i][:], t["gq", i][:], OP.mult)

        def f_dcr(i):
            g, js = rows(i)
            stt(t["dz", g, H][:, js, :], t["c2", i][:], -1.0, t["r", i][:], OP.mult, OP.mult)

        def f_drg(i):
            g, js = rows(i)
            tt(t["dz", g, R][:, js, :], t["c2", i][:], t["t1", i][:], OP.mult)

        def transpose(i, q):
            g, js = rows(i)
            bank = psum.tile([P, 2, 2 * P], F32, name="tr", tag="tr", bufs=2)
            t["tr", i, q] = bank
            for j in range(J):
                words = t["dz", g, q][:, js.start + j, :].bitcast(F32)
                for u in range(2):
                    nc.tensor.transpose(bank[:, u, j * P : (j + 1) * P], words[:, u : C // 2 : 2], id_f[:])

        def evac(i, q):
            if q == H:
                t["dzT", i, H] = mx.tile([P, 1, 2 * P, 4], BF16, name="dzTh", tag="dzTh", bufs=2, align_bytes=64)
            elif ("dzT", i, Z) not in t:
                t["dzT", i, Z] = mx.tile([P, 2, 2 * P, 4], BF16, name="dzTp", tag="wide", bufs=4, align_bytes=64)
                t["dzT", i, R] = t["dzT", i, Z]
            k = 1 if q == R else 0
            nc.scalar.copy(
                out=t["dzT", i, q][:, k, :, :].bitcast(F32), in_=t["tr", i, q][:].rearrange("p u r -> p r u")
            )

        def quant_f(i, gates):
            n = len(gates)
            codes = mx.tile([P, n, 2 * P], U32, name="f_codes", tag="f_codes%d" % n, bufs=3, align_bytes=64)
            scales = mx.tile([P, n, 2 * P], U8, name="f_scales", tag="f_scales%d" % n, bufs=3, align_bytes=64)
            for k, q in enumerate(gates):
                t["fc", i, q], t["fs", i, q] = codes[:, k, :], scales[:, k, :]
            nc.vector.quantize_mx(
                out=codes[:].rearrange("p n r -> p (n r)").bitcast(E5X4),
                scales=scales[:].rearrange("p n r -> p (n r)"),
                in_=t["dzT", i, gates[0]][:].rearrange("p n r t -> p (n r t)"),
            )

        def mm_0_tile(i, j, gates, first, last):
            if first:
                t["o0", i, j] = psum.tile([P, C], F32, name="o0", tag="o0", bufs=2)
            cols = slice(j * P, (j + 1) * P)
            for n, q in enumerate(gates):
                nc.tensor.matmul_mx(
                    t["o0", i, j][:],
                    lhsT=t["fc", i, q][:, cols].bitcast(E5X4),
                    lhsT_scale=t["fs", i, q][:, cols],
                    rhs=w_codes[q][:].bitcast(E4X4),
                    rhs_scale=w_scales[q][:],
                    start=(first and n == 0),
                    stop=(last and n == len(gates) - 1),
                )

        def mm_0(i):
            for j in range(J):
                mm_0_tile(i, j, (Z, R, H), True, True)

        def fin_0(i):
            g, js = rows(i)
            for j in range(J):
                tt(t["gz", i][:, j, :], t["o0", i, j][:], t["gz", i][:, j, :], OP.add)
            nc.sync.dma_start(out=o_v[g][:, js, :], in_=t["gz", i][:])

        def fin_0j(i, j):
            g, js = rows(i)
            tt(t["gz", i][:, j, :], t["o0", i, j][:], t["gz", i][:, j, :], OP.add)
            nc.sync.dma_start(out=o_v[g][:, js.start + j, :], in_=t["gz", i][:, j, :])

        def interleave(copy, src, key, cols=slice(0, C)):
            if key not in t:
                t[key] = mx.tile([P, C, 4], BF16, name="ilv", tag="ilv", bufs=3, align_bytes=64)
            copy(
                out=t[key][:, cols, :].rearrange("p (c i) t -> p c t i", i=4),
                in_=src[:, :, cols].rearrange("p t (c i) -> p c t i", i=4),
            )

        def quant_t(key, codes, scales, dt):
            nc.vector.quantize_mx(
                out=codes[:].bitcast(dt), scales=scales[:], in_=t[key][:].rearrange("p w j -> p (w j)")
            )

        def ilv_dz(g, q):
            interleave(nc.scalar.copy, t["dz", g, q], ("ilv", g, q))

        def quant_dz(g, q):
            quant_t(("ilv", g, q), tok_codes[g, q], tok_scales[g, q], E5X4)

        def ilv_h(g):
            interleave(nc.scalar.copy, t["h", g], ("ilvh", g))

        def quant_h(g):
            quant_t(("ilvh", g), h_codes[g], h_scales[g], E4X4)

        def mm_1(q, m, g, bank, start, stop):
            cols = slice(m * P, (m + 1) * P)
            nc.tensor.matmul_mx(
                bank[:],
                lhsT=h_codes[g][:, cols].bitcast(E4X4),
                lhsT_scale=h_scales[g][:, cols],
                rhs=tok_codes[g, q][:].bitcast(E5X4),
                rhs_scale=tok_scales[g, q][:],
                start=start,
                stop=stop,
            )

        def fin_1(q, m, bank):
            if m == 0:
                t["res", q] = inp.tile([P, 4, C], F32, name="res1", tag="mh")
            nc.scalar.copy(out=t["res", q][:, m, :], in_=bank[:])

        def add_1(q, m, bank):
            tt(t["res", q][:, m, :], bank[:], t["res", q][:, m, :], OP.add)

        def store_1(q, m):
            nc.sync.dma_start(out=out_1[m * P : (m + 1) * P, gate(q)], in_=t["res", q][:, m, :])

        def pass_1(q, groups, first, last, ms=range(4), tag="pa"):
            for m in ms:
                if first:
                    t["b1", q, m] = psum.tile([P, C], F32, name="pa", tag=tag, bufs=4 if tag == "pa" else 2)
                for n, gg in enumerate(groups):
                    mm_1(q, m, gg, t["b1", q, m], first and n == 0, last and n == len(groups) - 1)

        def w_transpose(q, half):
            bank = psum.tile([P, 2, 2 * P], F32, name="tr", tag="tr", bufs=2)
            for b in range(2):
                words = t["w"][:, 2 * half + b, gate(q)].bitcast(F32)
                for u in range(2):
                    nc.tensor.transpose(bank[:, u, b * P : (b + 1) * P], words[:, u : C // 2 : 2], id_f[:])
            if half == 0:
                t["wT", q] = mx.tile([P, C, 4], BF16, name="wT", tag="wide", bufs=4, align_bytes=64)
            nc.scalar.copy(
                out=t["wT", q][:, half * 2 * P : (half + 1) * 2 * P, :].bitcast(F32),
                in_=bank[:].rearrange("p u r -> p r u"),
            )

        def w_quant(q):
            quant_t(("wT", q), w_codes[q], w_scales[q], E4X4)

        pe_r = {1: (0,),2: (0,1),3: (0,1),4: (0,1),5: (0,1),6: (0,1),7: (0,)}

        def tiles_g(i):
            gate_tile("r", i + 1)
            gate_tile("q", i + 1)
            if i % 2 == 0:
                dz_tiles(i // 2)
            if i > 0:
                mid_tiles(i)

        def r_v(n):
            js = [j for j in range(J) if j not in pe_r.get(n, ())]
            if len(js) == J:
                v_add("r", R, n)
            else:
                for j in js:
                    v_add("r", R, n, j)

        def r_sig(n):
            js = [j for j in range(J) if j not in pe_r.get(n, ())]
            if len(js) == J:
                sig("r", n)
            else:
                for j in js:
                    sig("r", n, j)

        def r_pe(n):
            for j in pe_r.get(n, ()):
                pe_add("r", R, n, j)

        def r_sigpe(n):
            for j in pe_r.get(n, ()):
                sig_pe("r", n, j)

        def ilvq(g, q, k):
            w = C // 2
            interleave(nc.scalar.copy, t["dz", g, q], ("ilv", g, q), slice(k * w, k * w + w))

        def ilvv(g, q, k):
            w = C // 2
            interleave(nc.vector.tensor_copy, t["dz", g, q], ("ilv", g, q), slice(k * w, k * w + w))

        def ilvh(g, k):
            w = C // 2
            interleave(nc.scalar.copy, t["h", g], ("ilvh", g), slice(k * w, k * w + w))

        A, B = CHUNKS - 2, CHUNKS - 1
        g = GROUPS - 1

        with tc.manual_schedule():
            alloc_in(0)
            alloc_in(1)
            alloc_in(2)
            load_first()
            load_gates(1, (Z, R))
            load_g(1)
            load_gates(1, (H,))
            load_hn(1)
            load_gates(2, (Z, R, H))
            gate_tile("r", 0)
            gate_tile("q", 0)
            mid_tiles(0)
            for j in range(J):
                v_add("r", R, 0, j)
                sig("r", 0, j)
            for j in range(J):
                f_t1(0, j)
            for j in range(J):
                f_ac(0, j)
                tanh(0, j)
            square(0)
            for j in range(J):
                v_add("q", Z, 0, j)
                sig("q", 0, j)
            f_v(0)
            t["w"] = inp.tile([P, 4, G], BF16, name="w", tag="mh")
            nc.sync.dma_start(out=t["w"][:], in_=w_v)
            load_g(2)
            load_hn(2)
            load_h(0)
            i = 0
            f_hm(i)
            z_sum(i + 1, 0)
            gate_tile("r", i + 1)
            gate_tile("q", i + 1)
            if i % 2 == 0:
                dz_tiles(i // 2)
            if i > 0:
                mid_tiles(i)
            f_gq(i)
            z_sum(i + 1, 1)
            f_dzg(i)
            f_ndc(i)
            z_sig(i + 1, 0)
            r_pe(i + 1)
            r_v(i + 1)
            f_drg(i)
            r_sig(i + 1)
            z_sig(i + 1, 1)
            z_back(i + 1, 0)
            transpose(i, R)
            r_sigpe(i + 1)
            transpose(i, Z)
            evac(i, R)
            f_gz(i)
            f_dcr(i)
            z_back(i + 1, 1)
            evac(i, Z)
            for i in range(1, CHUNKS - 2):
                transpose(i - 1, H)
                if i % 2 == 0 and i > 1:
                    ilvq(i // 2 - 1, Z, 0)
                if i == 3:
                    fin_0(0)
                if i > 3:
                    fin_0(i - 2)
                gate_tile("r", i + 1)
                gate_tile("q", i + 1)
                if i % 2 == 0:
                    dz_tiles(i // 2)
                if i > 0:
                    mid_tiles(i)
                if i % 2 == 1 and i > 1:
                    ilvq(i // 2 - 1, R, 0)
                if i < 3:
                    f_t1(i, 1)
                if i % 2 == 0 and i > 1:
                    ilvq(i // 2 - 1, H, 0)
                f_gq(i)
                f_t1(i, ALL if i > 2 else 0, nc.gpsimd)
                if i == 3:
                    mm_0(1)
                if i > 2:
                    quant_h(i - 3)
                if i % 2 == 0 and i > 1:
                    ilvq(i // 2 - 1, Z, 1)
                z_sum(i + 1, 0)
                f_ac(i)
                evac(i - 1, H)
                tanh(i)
                r_pe(i + 1)
                square(i)
                z_sig(i + 1, 0)
                if i % 2 == 0 and i > 1:
                    quant_dz(i // 2 - 1, Z)
                if i % 2 == 1 and i > 1:
                    quant_dz(i // 2 - 1, H)
                if i == 3:
                    fin_0(1)
                if i % 2 == 1 and i > 1:
                    ilvq(i // 2 - 1, R, 1)
                alloc_in(i + 2)
                load(i + 2)
                if i == 2:
                    w_quant(Z)
                if i == 1:
                    w_transpose(Z, 0)
                    w_transpose(Z, 1)
                r_v(i + 1)
                f_v(i)
                quant_f(i - 1, (H,))
                if i == 2:
                    w_transpose(R, 0)
                    w_transpose(R, 1)
                quant_f(i - 1, (Z, R))
                z_sum(i + 1, 1)
                f_hm(i)
                f_ndc(i)
                if i == 2:
                    w_quant(R)
                if i > 2:
                    mm_0(i - 1)
                f_dzg(i)
                f_drg(i)
                if i > 1:
                    ilvh(i - 2, 0)
                r_sig(i + 1)
                if i == 2:
                    w_transpose(H, 0)
                    w_transpose(H, 1)
                z_back(i + 1, 0)
                transpose(i, Z)
                if i == 2:
                    w_quant(H)
                if i == 2:
                    mm_0(0)
                z_sig(i + 1, 1)
                if i > 1:
                    ilvh(i - 2, 1)
                    if i < 5:
                        load_h(i - 1)
                evac(i, Z)
                if i % 2 == 1 and i > 1:
                    quant_dz(i // 2 - 1, R)
                f_dcr(i)
                r_sigpe(i + 1)
                f_gz(i)
                transpose(i, R)
                evac(i, R)
                z_back(i + 1, 1)
                if i % 2 == 0 and i > 1:
                    ilvq(i // 2 - 1, H, 1)
            i = A
            z_sum(i + 1, 1)
            z_sum(i + 1, 0)
            ilvq(i // 2 - 1, R, 0)
            ilvq(i // 2 - 1, R, 1)
            fin_0(i - 2)
            gate_tile("r", B)
            gate_tile("q", B)
            dz_tiles(g)
            mid_tiles(A)
            f_t1(A, ALL, nc.gpsimd)
            z_sig(i + 1, 0)
            f_gq(A)
            r_pe(i + 1)
            transpose(i - 1, H)
            f_ac(A)
            z_sig(i + 1, 1)
            r_v(i + 1)
            tanh(A)
            mid_tiles(B)
            r_sig(i + 1)
            quant_h(g)
            f_gz(A)
            z_back(i + 1, 1)
            z_back(i + 1, 0)
            quant_dz(i // 2 - 1, R)
            quant_f(i - 1, (Z, R))
            square(A)
            r_sigpe(i + 1)
            f_hm(A)
            f_t1(B, ALL, nc.gpsimd)
            ilvq(i // 2 - 1, Z, 1)
            ilvq(i // 2 - 1, H, 0)
            ilvq(i // 2 - 1, H, 1)
            f_gq(B)
            f_dzg(A)
            f_ac(B)
            evac(i - 1, H)
            quant_f(i - 1, (H,))
            tanh(B)
            pass_1(R, range(3), True, True)
            square(B)
            mm_0(i - 1)
            f_ndc(A)
            ilvq(i // 2 - 1, Z, 0)
            fin_1(R, 0, t["b1", R, 0])
            fin_1(R, 2, t["b1", R, 2])
            fin_0(B - 2)
            fin_1(R, 1, t["b1", R, 1])
            transpose(A, Z)
            f_hm(B)
            quant_dz(i // 2 - 1, Z)
            fin_1(R, 3, t["b1", R, 3])
            f_dzg(B)
            evac(A, Z)
            f_ndc(B)
            f_dcr(A)
            ilvq(g, Z, 1)
            f_dcr(B)
            ilvq(g, Z, 0)
            pass_1(Z, range(3), True, False)
            quant_dz(g, Z)
            transpose(B, Z)
            f_v(A)
            ilvq(g, H, 1)
            pass_1(Z, (3,), False, True)
            evac(B, Z)
            f_v(B)
            quant_dz(i // 2 - 1, H)
            transpose(A, H)
            transpose(B, H)
            fin_1(Z, 0, t["b1", Z, 0])
            store_1(Z, 0)
            fin_1(Z, 3, t["b1", Z, 3])
            store_1(Z, 3)
            fin_1(Z, 2, t["b1", Z, 2])
            store_1(Z, 2)
            fin_1(Z, 1, t["b1", Z, 1])
            store_1(Z, 1)
            evac(B, H)
            evac(A, H)
            f_drg(B)
            f_drg(A)
            pass_1(H, range(3), True, False, (0, 1))
            f_gz(B)
            ilvq(g, H, 0)
            pass_1(H, range(3), True, False, (2, 3))
            quant_dz(g, H)
            ilvv(g, R, 1)
            transpose(A, R)
            ilvq(g, R, 0)
            evac(A, R)
            pass_1(H, (3,), False, True)
            quant_f(A, (H,))
            fin_1(H, 0, t["b1", H, 0])
            store_1(H, 0)
            quant_dz(g, R)
            quant_f(B, (H,))
            quant_f(A, (Z, R))
            fin_1(H, 2, t["b1", H, 2])
            store_1(H, 2)
            transpose(B, R)
            evac(B, R)
            pass_1(R, (3,), True, True, (3,), "pa")
            add_1(R, 3, t["b1", R, 3])
            store_1(R, 3)
            fin_1(H, 1, t["b1", H, 1])
            store_1(H, 1)
            fin_1(H, 3, t["b1", H, 3])
            store_1(H, 3)
            for j in range(J):
                mm_0_tile(A, j, (H,), True, False)
            for j in range(J):
                mm_0_tile(A, j, (Z, R), False, True)
            quant_f(B, (Z, R))
            fin_0(A)
            pass_1(R, (3,), True, True, (1,), "tr")
            add_1(R, 1, t["b1", R, 1])
            store_1(R, 1)
            pass_1(R, (3,), True, True, (0,), "tr")
            add_1(R, 0, t["b1", R, 0])
            store_1(R, 0)
            mm_0(B)
            for j in range(J):
                fin_0j(B, j)
            pass_1(R, (3,), True, True, (2,), "pa")
            add_1(R, 2, t["b1", R, 2])
            store_1(R, 2)
